import numpy as np
import ml_dtypes


def mxq(x, axis, fmt="e4m3"):
    dtype, down = {"e4m3": (ml_dtypes.float8_e4m3fn, 7), "e5m2": (ml_dtypes.float8_e5m2, 14)}[fmt]
    v = np.moveaxis(np.asarray(x, np.float32).astype(ml_dtypes.bfloat16).astype(np.float64), axis, -1)
    blocks = v.reshape(v.shape[:-1] + (-1, 32))
    amax = np.abs(blocks).max(-1, keepdims=True)
    byte = np.maximum(np.where(amax > 0, np.frexp(amax)[1] - 1 + 127, 0) - down, 1)
    scale = np.exp2(byte - 127.0)
    codes = (blocks / scale).astype(np.float32).astype(dtype).astype(np.float64)
    return np.moveaxis((codes * scale).reshape(v.shape), -1, axis)


WIDE = False


def mx_kscale(k):
    if not WIDE:
        return np.ones(k)
    levels = np.array([10, -10, 5, -5, 0])
    if k % 512:
        return np.exp2(np.random.permutation(np.resize(levels, k // 32))).repeat(32)
    a = np.empty((k // 512, 16))
    for p in range(k // 512):
        a[p, :8] = np.random.permutation(np.resize(levels, 8))
        for g in range(8):
            far = levels[np.abs(levels - a[p, g]) >= 10]
            a[p, g + 8] = far[np.random.randint(len(far))]
    return np.exp2(a.ravel()).repeat(32)


BF16 = ml_dtypes.bfloat16


def bf(x):
    return np.asarray(x, np.float32).astype(BF16)


def f64(x):
    return np.asarray(x).astype(np.float64)


B, S, HID, NH, NKV, HD, FF = 1, 512, 2048, 16, 4, 128, 8192
T = B * S
EPS = 1e-6


def rms(u, w):
    return u * (1.0 / np.sqrt(np.mean(u * u, axis=-1, keepdims=True) + EPS)) * w


def rotate_half(u):
    u1, u2 = np.split(u, 2, axis=-1)
    return np.concatenate([-u2, u1], axis=-1)


def setup_inputs():
    s = mx_kscale(HID)
    pos = np.tile(np.arange(S, dtype=np.float64), B)
    inv_freq = 1.0 / (10000.0 ** (np.arange(0, HD, 2, dtype=np.float64) / HD))
    ang = pos[:, None] * inv_freq[None, :]
    emb = np.concatenate([ang, ang], axis=-1)
    a = 1.0 / np.sqrt(HID)
    return {"x": bf(np.random.standard_normal((T, HID)) * 0.5),
            "cos": bf(np.cos(emb)),
            "sin": bf(np.sin(emb)),
            "wq": bf(np.random.standard_normal((NH * HD, HID)) * a / s[None, :]),
            "bq": bf(np.random.standard_normal(NH * HD) * 0.3),
            "wk": bf(np.random.standard_normal((NKV * HD, HID)) * a / s[None, :]),
            "bk": bf(np.random.standard_normal(NKV * HD) * 0.3),
            "wv": bf(np.random.standard_normal((NKV * HD, HID)) * 2.0 * a / s[None, :]),
            "bv": bf(np.random.standard_normal(NKV * HD) * 0.3),
            "q_norm_w": bf(1.0 + 0.1 * np.random.standard_normal(HD)),
            "k_norm_w": bf(1.0 + 0.1 * np.random.standard_normal(HD)),
            "ln1_w": bf((1.0 + 0.1 * np.random.standard_normal(HID)) * s)}


def reference(x, cos, sin, wq, bq, wk, bk, wv, bv, q_norm_w, k_norm_w, ln1_w):
    h = rms(f64(x), f64(ln1_w))
    hq = mxq(h, 1, "e4m3")
    q = ((hq @ mxq(f64(wq), 1, "e4m3").T) + f64(bq)).reshape(T, NH, HD)
    k = ((hq @ mxq(f64(wk), 1, "e4m3").T) + f64(bk)).reshape(T, NKV, HD)
    v = ((hq @ mxq(f64(wv), 1, "e4m3").T) + f64(bv)).reshape(T, NKV, HD)
    q = rms(q, f64(q_norm_w))
    k = rms(k, f64(k_norm_w))
    c, sn = f64(cos)[:, None, :], f64(sin)[:, None, :]
    q = q * c + rotate_half(q) * sn
    k = k * c + rotate_half(k) * sn
    return q, k, v

@@ -1,0 +1,406 @@
+from contextlib import ExitStack
+
+import concourse.mybir as mybir
+from concourse.masks import make_identity
+
+F32 = mybir.dt.float32
+BF16 = mybir.dt.bfloat16
+I32 = mybir.dt.int32
+U32 = mybir.dt.uint32
+U8 = mybir.dt.uint8
+FP8X4 = mybir.dt.float8_e4m3fn_x4
+ACT = mybir.ActivationFunctionType
+ALU = mybir.AluOpType
+
+P = 128
+TOKENS = 512
+HID = 2048
+HEAD = 128
+HALF = HEAD // 2
+EPS = 1e-6
+
+TOKEN_TILES = TOKENS // P
+PACK = 4
+K_PASS = P * PACK
+PASSES = HID // K_PASS
+PAIR = 2
+WORDS = PACK // PAIR
+GROUP = 512
+GROUP_HEADS = GROUP // HEAD
+ROW_TILES = GROUP // P
+Q_GROUPS = 4
+K_GROUP = 4
+V_GROUP = 5
+GROUPS = 6
+
+WEIGHT_BUFS = 4
+RING_BANKS = 6
+UNIT_BANKS = 2
+RUN_AHEAD = RING_BANKS // UNIT_BANKS
+H_BLOCKS = PACK * PASSES // UNIT_BANKS
+BANK_ROW_TILES = ROW_TILES // UNIT_BANKS
+
+FLOPS = 2 * TOKENS * HID * GROUPS * GROUP
+
+
+def tile_qwen2decoderlayer_pa_kernel(
+    tc, x, cos, sin, wq, bq, wk, bk, wv, bv, q_norm_w, k_norm_w, ln1_w, out_0, out_1, out_2
+):
+    nc = tc.nc
+
+    weight_rows = [wq[n * GROUP : (n + 1) * GROUP, :] for n in range(Q_GROUPS)] + [wk, wv]
+    bias_rows = [bq[n * GROUP : (n + 1) * GROUP] for n in range(Q_GROUPS)] + [bk, bv]
+    q_flat = out_0.rearrange("m a d -> m (a d)")
+    out_cols = [q_flat[:, n * GROUP : (n + 1) * GROUP] for n in range(Q_GROUPS)] + [
+        out_1.rearrange("m a d -> m (a d)"),
+        out_2.rearrange("m a d -> m (a d)"),
+    ]
+
+    with ExitStack() as ctx:
+        ctx.enter_context(tc.manual_schedule())
+        const = ctx.enter_context(tc.tile_pool(name="const", bufs=1))
+        hpool = ctx.enter_context(tc.tile_pool(name="hpool", bufs=2))
+        wpool = ctx.enter_context(tc.tile_pool(name="wpool", bufs=WEIGHT_BUFS))
+        gpool = ctx.enter_context(tc.tile_pool(name="gpool", bufs=6))
+        cpool = ctx.enter_context(tc.tile_pool(name="cpool", bufs=2))
+        epool = ctx.enter_context(tc.tile_pool(name="epool", bufs=2))
+        stats = ctx.enter_context(tc.tile_pool(name="stats", bufs=2))
+        ring = ctx.enter_context(tc.psum_pool(name="ring", bufs=RING_BANKS))
+        rope_psum = ctx.enter_context(tc.psum_pool(name="rope_psum", bufs=1))
+
+        x_sb = const.tile([P, TOKEN_TILES, HID], BF16)
+        nc.sync.dma_start(out=x_sb[:, 0, :], in_=x[0:P, :])
+        lnw_row = const.tile([P, HID], BF16)
+        nc.vector.memset(lnw_row[:].bitcast(I32), 0)
+        nc.sync.dma_start(out=lnw_row[0:1, :], in_=ln1_w.unsqueeze(0))
+        for i in range(1, TOKEN_TILES):
+            nc.sync.dma_start(out=x_sb[:, i, :], in_=x[i * P : (i + 1) * P, :])
+        cos_sb = const.tile([P, TOKEN_TILES, HEAD], BF16)
+        nc.sync.dma_start(out=cos_sb[:], in_=cos.rearrange("(i p) d -> p i d", p=P))
+        sin_sb = const.tile([P, TOKEN_TILES, HEAD], BF16)
+        nc.sync.dma_start(out=sin_sb[:], in_=sin.rearrange("(i p) d -> p i d", p=P))
+        gain_q = const.tile([P, HEAD], BF16)
+        nc.sync.dma_start(out=gain_q[:], in_=q_norm_w.partition_broadcast(P))
+        gain_k = const.tile([P, HEAD], BF16)
+        nc.sync.dma_start(out=gain_k[:], in_=k_norm_w.partition_broadcast(P))
+
+        bias = const.tile([P, GROUPS * GROUP], BF16)
+        w_sb = {}
+
+        def load_weights(n):
+            w_rows = wpool.tile([P, ROW_TILES, HID], BF16)
+            nc.sync.dma_start(out=w_rows[:], in_=weight_rows[n].rearrange("(r p) k -> p r k", p=P))
+            nc.sync.dma_start(
+                out=bias[:, n * GROUP : (n + 1) * GROUP], in_=bias_rows[n].partition_broadcast(P)
+            )
+            w_sb[n] = w_rows
+
+        for n in range(WEIGHT_BUFS):
+            load_weights(n)
+
+        ident_bf = const.tile([P, P], BF16)
+        make_identity(nc, ident_bf[:])
+        ident_f = const.tile([P, P], F32)
+        make_identity(nc, ident_f[:])
+        eps = const.tile([P, 1], F32)
+        nc.vector.memset(eps[:], EPS)
+        warm = const.tile([P, 1], F32)
+        nc.scalar.activation(out=warm[:], in_=eps[:], func=ACT.Sqrt)
+        squares = const.tile([P, HID], BF16)
+
+        def rope_tables(gain, name):
+            swapped = const.tile([P, HEAD], BF16, name="swapped_" + name)
+            nc.gpsimd.tensor_scalar(
+                out=swapped[:, 0:HALF], in0=gain[:, HALF:HEAD], scalar1=-1.0, scalar2=0.0,
+                op0=ALU.mult, op1=ALU.add,
+            )
+            nc.gpsimd.tensor_scalar(
+                out=swapped[:, HALF:HEAD], in0=gain[:, 0:HALF], scalar1=1.0, scalar2=0.0,
+                op0=ALU.mult, op1=ALU.add,
+            )
+            cos_gain = const.tile([P, TOKEN_TILES, HEAD], F32, name="cos_gain_" + name)
+            nc.gpsimd.tensor_tensor(
+                out=cos_gain[:], in0=cos_sb[:],
+                in1=gain[:].unsqueeze(1).to_broadcast([P, TOKEN_TILES, HEAD]), op=ALU.mult,
+            )
+            sin_gain = const.tile([P, TOKEN_TILES, HEAD], F32, name="sin_gain_" + name)
+            nc.gpsimd.tensor_tensor(
+                out=sin_gain[:], in0=sin_sb[:],
+                in1=swapped[:].unsqueeze(1).to_broadcast([P, TOKEN_TILES, HEAD]), op=ALU.mult,
+            )
+            return cos_gain, sin_gain
+
+        tables_q = rope_tables(gain_q, "q")
+        tables_k = rope_tables(gain_k, "k")
+
+        def tables_to_psum(tables):
+            in_psum = []
+            for table, tag in zip(tables, ("cos", "sin")):
+                bank = rope_psum.tile([P, TOKEN_TILES, HEAD], F32, tag=tag, name="rope_" + tag)
+                nc.tensor.matmul(
+                    out=bank[:].rearrange("p i d -> p (i d)"), lhsT=ident_f[:],
+                    rhs=table[:].rearrange("p i d -> p (i d)"), start=True, stop=True,
+                )
+                in_psum.append(bank)
+            return in_psum
+
+        h_codes = const.tile([P, TOKEN_TILES, PASSES, P], U32, align_bytes=64)
+        h_scales = const.tile([P, TOKEN_TILES, PASSES, P], U8, align_bytes=64)
+        x_ss = const.tile([P, TOKEN_TILES], F32)
+        x_rms = const.tile([P, TOKEN_TILES], F32)
+        x_rstd = const.tile([P, TOKEN_TILES], F32)
+
+        ones = const.tile([P, P], BF16)
+        nc.vector.memset(ones[:], 1.0)
+        lnw = const.tile([P, HID], BF16)
+        for chunk in range(HID // GROUP):
+            cols = slice(chunk * GROUP, (chunk + 1) * GROUP)
+            spread = ring.tile([P, GROUP], F32, tag="bank")
+            nc.tensor.matmul(out=spread[:], lhsT=ones[:], rhs=lnw_row[:, cols], start=True, stop=True)
+            nc.vector.tensor_copy(out=lnw[:, cols], in_=spread[:])
+        lnw_packs = lnw[:].rearrange("p (g j t) -> p g j t", j=P, t=PACK)
+
+        h_tiles = {}
+        h_banks = {}
+        grouped_h = {}
+
+        def x_stats(i):
+            nc.scalar.activation(
+                out=squares[:], in_=x_sb[:, i, :], func=ACT.Square, accum_out=x_ss[:, i : i + 1]
+            )
+            nc.scalar.activation(
+                out=x_rms[:, i : i + 1], in_=x_ss[:, i : i + 1], func=ACT.Sqrt,
+                scale=1.0 / HID, bias=eps[:, 0:1],
+            )
+
+        def x_scale(i):
+            nc.vector.reciprocal(out=x_rstd[:, i : i + 1], in_=x_rms[:, i : i + 1])
+            h_tile = hpool.tile([P, PASSES, PACK, P], BF16)
+            x_packs = x_sb[:, i, :].rearrange("p (g j t) -> p g j t", j=P, t=PACK)
+            for t in range(PACK):
+                nc.vector.scalar_tensor_tensor(
+                    out=h_tile[:, :, t, :], in0=x_packs[:, :, :, t], scalar=x_rstd[:, i : i + 1],
+                    in1=lnw_packs[:, :, :, t], op0=ALU.mult, op1=ALU.mult,
+                )
+            h_tiles[i] = h_tile
+
+        def x_transpose(i):
+            for half in range(UNIT_BANKS):
+                h_t = ring.tile([P, H_BLOCKS, P], BF16, tag="bank")
+                for b in range(H_BLOCKS):
+                    g, t = divmod(half * H_BLOCKS + b, PACK)
+                    nc.tensor.transpose(h_t[:, b, :], h_tiles[i][:, g, t, :], ident_bf[:])
+                h_banks[(i, half)] = h_t
+
+        def x_copy_out(i):
+            copy = nc.vector.tensor_copy if i == TOKEN_TILES - 1 else nc.scalar.copy
+            grouped = gpool.tile([P, GROUP * PACK], BF16, align_bytes=64, tag="grouped")
+            grouped_view = grouped[:].rearrange("p (g m t) -> p g m t", g=PASSES, t=PACK)
+            bank_passes = PASSES // UNIT_BANKS
+            for half in range(UNIT_BANKS):
+                copy(
+                    out=grouped_view[:, half * bank_passes : (half + 1) * bank_passes, :, :],
+                    in_=h_banks[(i, half)][:].rearrange("p (g t) m -> p g m t", t=PACK),
+                )
+            grouped_h[i] = grouped
+
+        def x_quantise(i):
+            nc.vector.quantize_mx(
+                out=h_codes[:, i, :, :].rearrange("p g m -> p (g m)").bitcast(FP8X4),
+                scales=h_scales[:, i, :, :].rearrange("p g m -> p (g m)"),
+                in_=grouped_h[i][:],
+            )
+
+        w_banks = {}
+        grouped_w = {}
+        w_codes = {}
+        w_scales = {}
+        sums = {}
+        u_sb = {}
+        rotated = {}
+        rms_sb = {}
+        rstd = {}
+
+        def transpose_weights(n, g):
+            for rp in range(UNIT_BANKS):
+                w_t = ring.tile([P, WORDS, BANK_ROW_TILES * P], F32, tag="bank")
+                for u in range(WORDS):
+                    for rr in range(BANK_ROW_TILES):
+                        first = (K_PASS // PAIR) * g + u
+                        last = (K_PASS // PAIR) * (g + 1)
+                        nc.tensor.transpose(
+                            w_t[:, u, rr * P : (rr + 1) * P],
+                            w_sb[n][:, BANK_ROW_TILES * rp + rr, :].bitcast(F32)[:, first:last:WORDS],
+                            ident_f[:],
+                        )
+                w_banks[(n, g, rp)] = w_t
+            if g == PASSES - 1 and n + WEIGHT_BUFS < GROUPS:
+                load_weights(n + WEIGHT_BUFS)
+
+        def copy_out_weights(n, g, copies):
+            grouped = gpool.tile([P, GROUP * PACK], BF16, align_bytes=64, tag="grouped")
+            grouped_words = grouped[:].bitcast(F32).rearrange("p (f u) -> p f u", u=WORDS)
+            bank_features = BANK_ROW_TILES * P
+            for rp, copy in enumerate(copies):
+                copy(
+                    out=grouped_words[:, rp * bank_features : (rp + 1) * bank_features, :],
+                    in_=w_banks[(n, g, rp)][:].rearrange("p u f -> p f u"),
+                )
+            grouped_w[(n, g)] = grouped
+
+        def quantise_weights(n, g):
+            if g == 0:
+                codes = cpool.tile([P, PASSES, GROUP], U32, align_bytes=64)
+                scales = cpool.tile([P, PASSES, GROUP], U8, align_bytes=64)
+                w_codes[n] = codes
+                w_scales[n] = scales
+            nc.vector.quantize_mx(
+                out=w_codes[n][:, g, :].bitcast(FP8X4), scales=w_scales[n][:, g, :],
+                in_=grouped_w[(n, g)][:],
+            )
+
+        def project(n):
+            for i in range(TOKEN_TILES):
+                bank = ring.tile([P, GROUP], F32, tag="bank")
+                for g in range(PASSES):
+                    nc.tensor.matmul_mx(
+                        out=bank[:],
+                        lhsT=h_codes[:, i, g, :].bitcast(FP8X4),
+                        lhsT_scale=h_scales[:, i, g, :],
+                        rhs=w_codes[n][:, g, :].bitcast(FP8X4),
+                        rhs_scale=w_scales[n][:, g, :],
+                        start=(g == 0),
+                        stop=(g == PASSES - 1),
+                    )
+                sums[(n, i)] = bank
+
+        def add_bias(n, i):
+            if i == 0:
+                u = epool.tile([P, TOKEN_TILES, GROUP_HEADS, HEAD], F32)
+                u_sb[n] = u
+            nc.vector.tensor_tensor(
+                out=u_sb[n][:, i, :, :].rearrange("p a d -> p (a d)"), in0=sums[(n, i)][:],
+                in1=bias[:, n * GROUP : (n + 1) * GROUP], op=ALU.add,
+            )
+
+        def head_rms(n):
+            ss = stats.tile([P, TOKEN_TILES * GROUP_HEADS], F32)
+            for i in range(TOKEN_TILES):
+                for head in range(GROUP_HEADS):
+                    col = i * GROUP_HEADS + head
+                    nc.scalar.activation(
+                        out=squares[:, col * HEAD : (col + 1) * HEAD], in_=u_sb[n][:, i, head, :],
+                        func=ACT.Square, accum_out=ss[:, col : col + 1],
+                    )
+            rms = stats.tile([P, TOKEN_TILES * GROUP_HEADS], F32)
+            nc.scalar.activation(out=rms[:], in_=ss[:], func=ACT.Sqrt, scale=1.0 / HEAD, bias=eps[:, 0:1])
+            rms_sb[n] = rms
+
+        def invert_rms(n):
+            inv = stats.tile([P, TOKEN_TILES * GROUP_HEADS], F32)
+            nc.vector.reciprocal(out=inv[:], in_=rms_sb[n][:])
+            rstd[n] = inv
+
+        def rotate(n, rope):
+            cos_gain, sin_gain = rope
+            u = u_sb[n]
+            shape = [P, TOKEN_TILES, GROUP_HEADS, HEAD]
+            half_shape = [P, TOKEN_TILES, GROUP_HEADS, HALF]
+            straight = epool.tile(shape, F32, bufs=3)
+            nc.vector.tensor_tensor(
+                out=straight[:], in0=u[:], in1=cos_gain[:].unsqueeze(2).to_broadcast(shape), op=ALU.mult
+            )
+            crossed = epool.tile(shape, F32)
+            nc.vector.tensor_tensor(
+                out=crossed[:, :, :, 0:HALF], in0=u[:, :, :, HALF:HEAD],
+                in1=sin_gain[:, :, 0:HALF].unsqueeze(2).to_broadcast(half_shape), op=ALU.mult,
+            )
+            nc.vector.tensor_tensor(
+                out=crossed[:, :, :, HALF:HEAD], in0=u[:, :, :, 0:HALF],
+                in1=sin_gain[:, :, HALF:HEAD].unsqueeze(2).to_broadcast(half_shape), op=ALU.mult,
+            )
+            for i in range(TOKEN_TILES):
+                nc.gpsimd.tensor_tensor(
+                    out=straight[:, i, :, :], in0=straight[:, i, :, :], in1=crossed[:, i, :, :], op=ALU.add
+                )
+            rotated[n] = straight
+
+        def scale_and_store(n):
+            for i in range(TOKEN_TILES):
+                for head in range(GROUP_HEADS):
+                    col = i * GROUP_HEADS + head
+                    nc.scalar.activation(
+                        out=rotated[n][:, i, head, :], in_=rotated[n][:, i, head, :], func=ACT.Copy,
+                        scale=rstd[n][:, col : col + 1],
+                    )
+                nc.sync.dma_start(
+                    out=out_cols[n][i * P : (i + 1) * P, :],
+                    in_=rotated[n][:, i, :, :].rearrange("p a d -> p (a d)"),
+                )
+
+        def store_plain(n):
+            for i in range(TOKEN_TILES):
+                nc.sync.dma_start(
+                    out=out_cols[n][i * P : (i + 1) * P, :],
+                    in_=u_sb[n][:, i, :, :].rearrange("p a d -> p (a d)"),
+                )
+
+        for i in range(TOKEN_TILES):
+            x_stats(i)
+        for i in range(TOKEN_TILES):
+            if i >= RUN_AHEAD:
+                x_copy_out(i - RUN_AHEAD)
+            x_scale(i)
+            x_transpose(i)
+        for i in range(TOKEN_TILES - RUN_AHEAD, TOKEN_TILES):
+            x_copy_out(i)
+
+        assert TOKEN_TILES == PASSES
+        for g in range(RUN_AHEAD):
+            transpose_weights(0, g)
+        for step in range(PASSES):
+            copy_out_weights(0, step, (nc.scalar.copy, nc.vector.tensor_copy))
+            if step + RUN_AHEAD < PASSES:
+                transpose_weights(0, step + RUN_AHEAD)
+            x_quantise(step)
+        for g in range(PASSES):
+            quantise_weights(0, g)
+
+        rope = tables_to_psum(tables_q)
+        for g in range(RUN_AHEAD):
+            transpose_weights(1, g)
+        for g in range(PASSES):
+            copy_out_weights(1, g, (nc.scalar.copy, nc.scalar.copy))
+            if g + RUN_AHEAD < PASSES:
+                transpose_weights(1, g + RUN_AHEAD)
+        project(0)
+
+        for n in range(GROUPS):
+            if n + 1 < GROUPS:
+                for g in range(PASSES):
+                    quantise_weights(n + 1, g)
+            for i in range(TOKEN_TILES):
+                add_bias(n, i)
+            if n >= 1:
+                invert_rms(n - 1)
+            if n + 2 < GROUPS:
+                for g in range(RUN_AHEAD):
+                    transpose_weights(n + 2, g)
+            if n == V_GROUP:
+                store_plain(n)
+            else:
+                head_rms(n)
+            if n + 2 < GROUPS:
+                for g in range(PASSES):
+                    first_copy = nc.vector.tensor_copy if g == 0 else nc.scalar.copy
+                    copy_out_weights(n + 2, g, (first_copy, nc.scalar.copy))
+                    if g + RUN_AHEAD < PASSES:
+                        transpose_weights(n + 2, g + RUN_AHEAD)
+            if n + 1 < GROUPS:
+                project(n + 1)
+            if n >= 1:
+                scale_and_store(n - 1)
+            if n != V_GROUP:
+                rotate(n, rope)
+            if n + 1 == K_GROUP:
+                rope = tables_to_psum(tables_k)

@@ -29,16 +29,20 @@ GROUP = 512
 GROUP_HEADS = GROUP // HEAD
 ROW_TILES = GROUP // P
 Q_GROUPS = 4
-K_GROUP = 4
-V_GROUP = 5
-GROUPS = 6
+GROUPS = Q_GROUPS + 2
+K_GROUP = 0
+V_GROUP = GROUPS - 1
+LAST_ROPE_GROUP = V_GROUP - 1
 
 WEIGHT_BUFS = 4
 RING_BANKS = 6
 UNIT_BANKS = 2
 RUN_AHEAD = RING_BANKS // UNIT_BANKS
-H_BLOCKS = PACK * PASSES // UNIT_BANKS
+BANK_PASSES = PASSES // UNIT_BANKS
 BANK_ROW_TILES = ROW_TILES // UNIT_BANKS
+BANK_BF16 = 1024
+ROTATE_TILES = 2
+SCALAR_TILES = (0, 1, 2)
 
 FLOPS = 2 * TOKENS * HID * GROUPS * GROUP
 
@@ -48,67 +52,183 @@ def tile_qwen2decoderlayer_pa_kernel(
 ):
     nc = tc.nc
 
-    weight_rows = [wq[n * GROUP : (n + 1) * GROUP, :] for n in range(Q_GROUPS)] + [wk, wv]
-    bias_rows = [bq[n * GROUP : (n + 1) * GROUP] for n in range(Q_GROUPS)] + [bk, bv]
     q_flat = out_0.rearrange("m a d -> m (a d)")
-    out_cols = [q_flat[:, n * GROUP : (n + 1) * GROUP] for n in range(Q_GROUPS)] + [
-        out_1.rearrange("m a d -> m (a d)"),
-        out_2.rearrange("m a d -> m (a d)"),
-    ]
+    q_slices = [slice(n * GROUP, (n + 1) * GROUP) for n in range(Q_GROUPS)]
+    weight_rows = [wk] + [wq[cols, :] for cols in q_slices] + [wv]
+    bias_rows = [bk] + [bq[cols] for cols in q_slices] + [bv]
+    out_cols = (
+        [out_1.rearrange("m a d -> m (a d)")]
+        + [q_flat[:, cols] for cols in q_slices]
+        + [out_2.rearrange("m a d -> m (a d)")]
+    )
 
     with ExitStack() as ctx:
         ctx.enter_context(tc.manual_schedule())
         const = ctx.enter_context(tc.tile_pool(name="const", bufs=1))
-        hpool = ctx.enter_context(tc.tile_pool(name="hpool", bufs=2))
+        hpool = ctx.enter_context(tc.tile_pool(name="hpool", bufs=TOKEN_TILES))
         wpool = ctx.enter_context(tc.tile_pool(name="wpool", bufs=WEIGHT_BUFS))
         gpool = ctx.enter_context(tc.tile_pool(name="gpool", bufs=6))
         cpool = ctx.enter_context(tc.tile_pool(name="cpool", bufs=2))
         epool = ctx.enter_context(tc.tile_pool(name="epool", bufs=2))
         stats = ctx.enter_context(tc.tile_pool(name="stats", bufs=2))
         ring = ctx.enter_context(tc.psum_pool(name="ring", bufs=RING_BANKS))
-        rope_psum = ctx.enter_context(tc.psum_pool(name="rope_psum", bufs=1))
+        table_psum = ctx.enter_context(tc.psum_pool(name="table_psum", bufs=1))
 
         x_sb = const.tile([P, TOKEN_TILES, HID], BF16)
         nc.sync.dma_start(out=x_sb[:, 0, :], in_=x[0:P, :])
         lnw_row = const.tile([P, HID], BF16)
         nc.vector.memset(lnw_row[:].bitcast(I32), 0)
         nc.sync.dma_start(out=lnw_row[0:1, :], in_=ln1_w.unsqueeze(0))
-        for i in range(1, TOKEN_TILES):
-            nc.sync.dma_start(out=x_sb[:, i, :], in_=x[i * P : (i + 1) * P, :])
-        cos_sb = const.tile([P, TOKEN_TILES, HEAD], BF16)
-        nc.sync.dma_start(out=cos_sb[:], in_=cos.rearrange("(i p) d -> p i d", p=P))
-        sin_sb = const.tile([P, TOKEN_TILES, HEAD], BF16)
-        nc.sync.dma_start(out=sin_sb[:], in_=sin.rearrange("(i p) d -> p i d", p=P))
-        gain_q = const.tile([P, HEAD], BF16)
-        nc.sync.dma_start(out=gain_q[:], in_=q_norm_w.partition_broadcast(P))
-        gain_k = const.tile([P, HEAD], BF16)
-        nc.sync.dma_start(out=gain_k[:], in_=k_norm_w.partition_broadcast(P))
+        nc.sync.dma_start(out=x_sb[:, 1, :], in_=x[P : 2 * P, :])
 
         bias = const.tile([P, GROUPS * GROUP], BF16)
         w_sb = {}
 
-        def load_weights(n):
-            w_rows = wpool.tile([P, ROW_TILES, HID], BF16)
-            nc.sync.dma_start(out=w_rows[:], in_=weight_rows[n].rearrange("(r p) k -> p r k", p=P))
+        def load_columns(n, first, last):
+            nc.sync.dma_start(
+                out=w_sb[n][:, :, first:last],
+                in_=weight_rows[n].rearrange("(r p) k -> p r k", p=P)[:, :, first:last],
+            )
+
+        def load_bias(n):
             nc.sync.dma_start(
                 out=bias[:, n * GROUP : (n + 1) * GROUP], in_=bias_rows[n].partition_broadcast(P)
             )
-            w_sb[n] = w_rows
 
-        for n in range(WEIGHT_BUFS):
+        def load_weights(n):
+            w_rows = wpool.tile([P, ROW_TILES, HID], BF16)
+            w_sb[n] = w_rows
+            load_columns(n, 0, HID)
+            load_bias(n)
+
+        w_rows = wpool.tile([P, ROW_TILES, HID], BF16)
+        w_sb[0] = w_rows
+        load_columns(0, 0, HID // 2)
+        for i in range(2, TOKEN_TILES):
+            nc.sync.dma_start(out=x_sb[:, i, :], in_=x[i * P : (i + 1) * P, :])
+        load_columns(0, HID // 2, HID)
+        cos_sin = const.tile([P, 2, TOKEN_TILES, HEAD], BF16)
+        nc.sync.dma_start(out=cos_sin[:, 0, :, :], in_=cos.rearrange("(i p) d -> p i d", p=P))
+        nc.sync.dma_start(out=cos_sin[:, 1, :, :], in_=sin.rearrange("(i p) d -> p i d", p=P))
+        gain_k = const.tile([P, HEAD], BF16)
+        nc.sync.dma_start(out=gain_k[:], in_=k_norm_w.partition_broadcast(P))
+        gain_q = const.tile([P, HEAD], BF16)
+        nc.sync.dma_start(out=gain_q[:], in_=q_norm_w.partition_broadcast(P))
+        load_bias(0)
+        for n in range(1, WEIGHT_BUFS):
             load_weights(n)
 
-        ident_bf = const.tile([P, P], BF16)
-        make_identity(nc, ident_bf[:])
         ident_f = const.tile([P, P], F32)
         make_identity(nc, ident_f[:])
+        ident_bf = const.tile([P, P], BF16)
+        make_identity(nc, ident_bf[:])
         eps = const.tile([P, 1], F32)
         nc.vector.memset(eps[:], EPS)
         warm = const.tile([P, 1], F32)
         nc.scalar.activation(out=warm[:], in_=eps[:], func=ACT.Sqrt)
         squares = const.tile([P, HID], BF16)
 
-        def rope_tables(gain, name):
+        ones = const.tile([P, P], BF16)
+        nc.vector.memset(ones[:], 1.0)
+        lnw_banks = []
+        for half in range(UNIT_BANKS):
+            bank = table_psum.tile([P, BANK_BF16], BF16, tag="table%d" % half, name="lnw_bank")
+            for first in range(0, BANK_BF16, GROUP):
+                nc.tensor.matmul(
+                    out=bank[:, first : first + GROUP], lhsT=ones[:],
+                    rhs=lnw_row[:, half * BANK_BF16 + first : half * BANK_BF16 + first + GROUP],
+                    start=True, stop=True,
+                )
+            lnw_banks.append(bank)
+        h_codes = const.tile([P, TOKEN_TILES, PASSES, P], U32, align_bytes=64)
+        h_scales = const.tile([P, TOKEN_TILES, PASSES, P], U8, align_bytes=64)
+        x_ss = const.tile([P, TOKEN_TILES], F32)
+        x_rms = const.tile([P, TOKEN_TILES], F32)
+        x_rstd = const.tile([P, TOKEN_TILES], F32)
+        x_gained = const.tile([P, HID], F32)
+        h_tiles = {}
+        banks = {}
+        grouped = {}
+
+        def x_squares_scalar(i):
+            nc.scalar.activation(
+                out=squares[:], in_=x_sb[:, i, :], func=ACT.Square, accum_out=x_ss[:, i : i + 1]
+            )
+
+        def x_squares_vector(i):
+            nc.vector.scalar_tensor_tensor(
+                out=x_gained[:].bitcast(BF16)[:, 0:HID], in0=x_sb[:, i, :], scalar=1.0, in1=x_sb[:, i, :],
+                op0=ALU.mult, op1=ALU.mult, accum_out=x_ss[:, i : i + 1],
+            )
+
+        def x_root(i):
+            nc.scalar.activation(
+                out=x_rms[:, i : i + 1], in_=x_ss[:, i : i + 1], func=ACT.Sqrt,
+                scale=1.0 / HID, bias=eps[:, 0:1],
+            )
+
+        def x_gain(i):
+            for half in range(UNIT_BANKS):
+                nc.vector.tensor_copy(
+                    out=lnw_row[:, half * BANK_BF16 : (half + 1) * BANK_BF16], in_=lnw_banks[half][:]
+                )
+            nc.gpsimd.tensor_tensor(out=x_gained[:], in0=x_sb[:, i, :], in1=lnw_row[:], op=ALU.mult)
+
+        def word_order(row):
+            return row.rearrange("p (g j u e) -> p u g j e", j=P, u=WORDS, e=PAIR)
+
+        def x_scale(i):
+            nc.vector.reciprocal(out=x_rstd[:, i : i + 1], in_=x_rms[:, i : i + 1])
+            h_tile = hpool.tile([P, PASSES, WORDS, P, PAIR], BF16)
+            for half in range(UNIT_BANKS):
+                x_words = word_order(x_sb[:, i, half * BANK_BF16 : (half + 1) * BANK_BF16])
+                lnw_words = word_order(lnw_banks[half][:])
+                for u in range(WORDS):
+                    nc.vector.scalar_tensor_tensor(
+                        out=h_tile[:, half * BANK_PASSES : (half + 1) * BANK_PASSES, u, :, :],
+                        in0=x_words[:, u, :, :, :], scalar=x_rstd[:, i : i + 1],
+                        in1=lnw_words[:, u, :, :, :], op0=ALU.mult, op1=ALU.mult,
+                    )
+            h_tiles[i] = h_tile
+
+        def x_scale_gained(i):
+            nc.vector.reciprocal(out=x_rstd[:, i : i + 1], in_=x_rms[:, i : i + 1])
+            h_tile = hpool.tile([P, PASSES, WORDS, P, PAIR], BF16)
+            gained_words = word_order(x_gained[:])
+            for u in range(WORDS):
+                nc.vector.tensor_scalar_mul(
+                    h_tile[:, :, u, :, :], gained_words[:, u, :, :, :], x_rstd[:, i : i + 1]
+                )
+            h_tiles[i] = h_tile
+
+        def transpose_h(i):
+            words = h_tiles[i][:].rearrange("p g u j e -> p (g u j e)").bitcast(F32)
+            for half in range(UNIT_BANKS):
+                h_t = ring.tile([P, BANK_PASSES, WORDS, P], F32, tag="bank")
+                for b in range(BANK_PASSES * WORDS):
+                    g, u = divmod(b, WORDS)
+                    first = (half * BANK_PASSES * WORDS + b) * P
+                    nc.tensor.transpose(h_t[:, g, u, :], words[:, first : first + P], ident_f[:])
+                banks[("h", i, half)] = h_t
+
+        def copy_h(i, copies):
+            tile = gpool.tile([P, GROUP * PACK], BF16, align_bytes=64, tag="grouped")
+            words = tile[:].bitcast(F32).rearrange("p (g m u) -> p g m u", g=PASSES, u=WORDS)
+            for half, copy in enumerate(copies):
+                copy(
+                    out=words[:, half * BANK_PASSES : (half + 1) * BANK_PASSES, :, :],
+                    in_=banks[("h", i, half)][:].rearrange("p g u m -> p g m u"),
+                )
+            grouped[("h", i)] = tile
+
+        def quantise_h(i):
+            nc.vector.quantize_mx(
+                out=h_codes[:, i, :, :].rearrange("p g m -> p (g m)").bitcast(FP8X4),
+                scales=h_scales[:, i, :, :].rearrange("p g m -> p (g m)"),
+                in_=grouped[("h", i)][:],
+            )
+
+        def diagonals(gain, name):
             swapped = const.tile([P, HEAD], BF16, name="swapped_" + name)
             nc.gpsimd.tensor_scalar(
                 out=swapped[:, 0:HALF], in0=gain[:, HALF:HEAD], scalar1=-1.0, scalar2=0.0,
@@ -118,106 +238,39 @@ def tile_qwen2decoderlayer_pa_kernel(
                 out=swapped[:, HALF:HEAD], in0=gain[:, 0:HALF], scalar1=1.0, scalar2=0.0,
                 op0=ALU.mult, op1=ALU.add,
             )
-            cos_gain = const.tile([P, TOKEN_TILES, HEAD], F32, name="cos_gain_" + name)
-            nc.gpsimd.tensor_tensor(
-                out=cos_gain[:], in0=cos_sb[:],
-                in1=gain[:].unsqueeze(1).to_broadcast([P, TOKEN_TILES, HEAD]), op=ALU.mult,
-            )
-            sin_gain = const.tile([P, TOKEN_TILES, HEAD], F32, name="sin_gain_" + name)
-            nc.gpsimd.tensor_tensor(
-                out=sin_gain[:], in0=sin_sb[:],
-                in1=swapped[:].unsqueeze(1).to_broadcast([P, TOKEN_TILES, HEAD]), op=ALU.mult,
-            )
-            return cos_gain, sin_gain
+            pair = const.tile([P, 2, HEAD], BF16, name="diagonals_" + name)
+            nc.gpsimd.tensor_tensor(out=pair[:, 0, :], in0=ident_bf[:], in1=gain[:], op=ALU.mult)
+            nc.gpsimd.tensor_tensor(out=pair[:, 1, :], in0=ident_bf[:], in1=swapped[:], op=ALU.mult)
+            return pair
 
-        tables_q = rope_tables(gain_q, "q")
-        tables_k = rope_tables(gain_k, "k")
+        turned = const.tile([P, 2, TOKEN_TILES, P], BF16)
 
-        def tables_to_psum(tables):
+        def turn_cos_sin():
+            bank = ring.tile([P, 2, TOKEN_TILES, P], BF16, tag="bank")
+            for half in range(2):
+                for i in range(TOKEN_TILES):
+                    nc.tensor.transpose(bank[:, half, i, :], cos_sin[:, half, i, :], ident_bf[:])
+            nc.scalar.copy(out=turned[:], in_=bank[:])
+
+        def rope_tables(pair):
             in_psum = []
-            for table, tag in zip(tables, ("cos", "sin")):
-                bank = rope_psum.tile([P, TOKEN_TILES, HEAD], F32, tag=tag, name="rope_" + tag)
-                nc.tensor.matmul(
-                    out=bank[:].rearrange("p i d -> p (i d)"), lhsT=ident_f[:],
-                    rhs=table[:].rearrange("p i d -> p (i d)"), start=True, stop=True,
-                )
+            for half in range(2):
+                bank = table_psum.tile([P, TOKEN_TILES, HEAD], F32, tag="table%d" % half, name="rope_bank")
+                for i in range(TOKEN_TILES):
+                    nc.tensor.matmul(
+                        out=bank[:, i, :], lhsT=turned[:, half, i, :], rhs=pair[:, half, :],
+                        start=True, stop=True,
+                    )
                 in_psum.append(bank)
             return in_psum
 
-        h_codes = const.tile([P, TOKEN_TILES, PASSES, P], U32, align_bytes=64)
-        h_scales = const.tile([P, TOKEN_TILES, PASSES, P], U8, align_bytes=64)
-        x_ss = const.tile([P, TOKEN_TILES], F32)
-        x_rms = const.tile([P, TOKEN_TILES], F32)
-        x_rstd = const.tile([P, TOKEN_TILES], F32)
-
-        ones = const.tile([P, P], BF16)
-        nc.vector.memset(ones[:], 1.0)
-        lnw = const.tile([P, HID], BF16)
-        for chunk in range(HID // GROUP):
-            cols = slice(chunk * GROUP, (chunk + 1) * GROUP)
-            spread = ring.tile([P, GROUP], F32, tag="bank")
-            nc.tensor.matmul(out=spread[:], lhsT=ones[:], rhs=lnw_row[:, cols], start=True, stop=True)
-            nc.vector.tensor_copy(out=lnw[:, cols], in_=spread[:])
-        lnw_packs = lnw[:].rearrange("p (g j t) -> p g j t", j=P, t=PACK)
-
-        h_tiles = {}
-        h_banks = {}
-        grouped_h = {}
-
-        def x_stats(i):
-            nc.scalar.activation(
-                out=squares[:], in_=x_sb[:, i, :], func=ACT.Square, accum_out=x_ss[:, i : i + 1]
-            )
-            nc.scalar.activation(
-                out=x_rms[:, i : i + 1], in_=x_ss[:, i : i + 1], func=ACT.Sqrt,
-                scale=1.0 / HID, bias=eps[:, 0:1],
-            )
-
-        def x_scale(i):
-            nc.vector.reciprocal(out=x_rstd[:, i : i + 1], in_=x_rms[:, i : i + 1])
-            h_tile = hpool.tile([P, PASSES, PACK, P], BF16)
-            x_packs = x_sb[:, i, :].rearrange("p (g j t) -> p g j t", j=P, t=PACK)
-            for t in range(PACK):
-                nc.vector.scalar_tensor_tensor(
-                    out=h_tile[:, :, t, :], in0=x_packs[:, :, :, t], scalar=x_rstd[:, i : i + 1],
-                    in1=lnw_packs[:, :, :, t], op0=ALU.mult, op1=ALU.mult,
-                )
-            h_tiles[i] = h_tile
-
-        def x_transpose(i):
-            for half in range(UNIT_BANKS):
-                h_t = ring.tile([P, H_BLOCKS, P], BF16, tag="bank")
-                for b in range(H_BLOCKS):
-                    g, t = divmod(half * H_BLOCKS + b, PACK)
-                    nc.tensor.transpose(h_t[:, b, :], h_tiles[i][:, g, t, :], ident_bf[:])
-                h_banks[(i, half)] = h_t
-
-        def x_copy_out(i):
-            copy = nc.vector.tensor_copy if i == TOKEN_TILES - 1 else nc.scalar.copy
-            grouped = gpool.tile([P, GROUP * PACK], BF16, align_bytes=64, tag="grouped")
-            grouped_view = grouped[:].rearrange("p (g m t) -> p g m t", g=PASSES, t=PACK)
-            bank_passes = PASSES // UNIT_BANKS
-            for half in range(UNIT_BANKS):
-                copy(
-                    out=grouped_view[:, half * bank_passes : (half + 1) * bank_passes, :, :],
-                    in_=h_banks[(i, half)][:].rearrange("p (g t) m -> p g m t", t=PACK),
-                )
-            grouped_h[i] = grouped
-
-        def x_quantise(i):
-            nc.vector.quantize_mx(
-                out=h_codes[:, i, :, :].rearrange("p g m -> p (g m)").bitcast(FP8X4),
-                scales=h_scales[:, i, :, :].rearrange("p g m -> p (g m)"),
-                in_=grouped_h[i][:],
-            )
-
-        w_banks = {}
-        grouped_w = {}
         w_codes = {}
         w_scales = {}
         sums = {}
         u_sb = {}
-        rotated = {}
+        straight = {}
+        crossed = {}
+        ss = {}
         rms_sb = {}
         rstd = {}
 
@@ -233,20 +286,20 @@ def tile_qwen2decoderlayer_pa_kernel(
                             w_sb[n][:, BANK_ROW_TILES * rp + rr, :].bitcast(F32)[:, first:last:WORDS],
                             ident_f[:],
                         )
-                w_banks[(n, g, rp)] = w_t
+                banks[(n, g, rp)] = w_t
             if g == PASSES - 1 and n + WEIGHT_BUFS < GROUPS:
                 load_weights(n + WEIGHT_BUFS)
 
-        def copy_out_weights(n, g, copies):
-            grouped = gpool.tile([P, GROUP * PACK], BF16, align_bytes=64, tag="grouped")
-            grouped_words = grouped[:].bitcast(F32).rearrange("p (f u) -> p f u", u=WORDS)
+        def copy_weights(n, g, copies):
+            tile = gpool.tile([P, GROUP * PACK], BF16, align_bytes=64, tag="grouped")
+            words = tile[:].bitcast(F32).rearrange("p (f u) -> p f u", u=WORDS)
             bank_features = BANK_ROW_TILES * P
             for rp, copy in enumerate(copies):
                 copy(
-                    out=grouped_words[:, rp * bank_features : (rp + 1) * bank_features, :],
-                    in_=w_banks[(n, g, rp)][:].rearrange("p u f -> p f u"),
+                    out=words[:, rp * bank_features : (rp + 1) * bank_features, :],
+                    in_=banks[(n, g, rp)][:].rearrange("p u f -> p f u"),
                 )
-            grouped_w[(n, g)] = grouped
+            grouped[(n, g)] = tile
 
         def quantise_weights(n, g):
             if g == 0:
@@ -256,23 +309,22 @@ def tile_qwen2decoderlayer_pa_kernel(
                 w_scales[n] = scales
             nc.vector.quantize_mx(
                 out=w_codes[n][:, g, :].bitcast(FP8X4), scales=w_scales[n][:, g, :],
-                in_=grouped_w[(n, g)][:],
+                in_=grouped[(n, g)][:],
             )
 
-        def project(n):
-            for i in range(TOKEN_TILES):
-                bank = ring.tile([P, GROUP], F32, tag="bank")
-                for g in range(PASSES):
-                    nc.tensor.matmul_mx(
-                        out=bank[:],
-                        lhsT=h_codes[:, i, g, :].bitcast(FP8X4),
-                        lhsT_scale=h_scales[:, i, g, :],
-                        rhs=w_codes[n][:, g, :].bitcast(FP8X4),
-                        rhs_scale=w_scales[n][:, g, :],
-                        start=(g == 0),
-                        stop=(g == PASSES - 1),
-                    )
-                sums[(n, i)] = bank
+        def project(n, i):
+            bank = ring.tile([P, GROUP], F32, tag="bank")
+            for g in range(PASSES):
+                nc.tensor.matmul_mx(
+                    out=bank[:],
+                    lhsT=h_codes[:, i, g, :].bitcast(FP8X4),
+                    lhsT_scale=h_scales[:, i, g, :],
+                    rhs=w_codes[n][:, g, :].bitcast(FP8X4),
+                    rhs_scale=w_scales[n][:, g, :],
+                    start=(g == 0),
+                    stop=(g == PASSES - 1),
+                )
+            sums[(n, i)] = bank
 
         def add_bias(n, i):
             if i == 0:
@@ -283,17 +335,20 @@ def tile_qwen2decoderlayer_pa_kernel(
                 in1=bias[:, n * GROUP : (n + 1) * GROUP], op=ALU.add,
             )
 
-        def head_rms(n):
-            ss = stats.tile([P, TOKEN_TILES * GROUP_HEADS], F32)
-            for i in range(TOKEN_TILES):
-                for head in range(GROUP_HEADS):
-                    col = i * GROUP_HEADS + head
-                    nc.scalar.activation(
-                        out=squares[:, col * HEAD : (col + 1) * HEAD], in_=u_sb[n][:, i, head, :],
-                        func=ACT.Square, accum_out=ss[:, col : col + 1],
-                    )
+        def head_squares(n, i):
+            if i == 0:
+                sums_of_squares = stats.tile([P, TOKEN_TILES * GROUP_HEADS], F32)
+                ss[n] = sums_of_squares
+            for head in range(GROUP_HEADS):
+                col = i * GROUP_HEADS + head
+                nc.scalar.activation(
+                    out=squares[:, col * HEAD : (col + 1) * HEAD], in_=u_sb[n][:, i, head, :],
+                    func=ACT.Square, accum_out=ss[n][:, col : col + 1],
+                )
+
+        def head_root(n):
             rms = stats.tile([P, TOKEN_TILES * GROUP_HEADS], F32)
-            nc.scalar.activation(out=rms[:], in_=ss[:], func=ACT.Sqrt, scale=1.0 / HEAD, bias=eps[:, 0:1])
+            nc.scalar.activation(out=rms[:], in_=ss[n][:], func=ACT.Sqrt, scale=1.0 / HEAD, bias=eps[:, 0:1])
             rms_sb[n] = rms
 
         def invert_rms(n):
@@ -301,106 +356,163 @@ def tile_qwen2decoderlayer_pa_kernel(
             nc.vector.reciprocal(out=inv[:], in_=rms_sb[n][:])
             rstd[n] = inv
 
-        def rotate(n, rope):
-            cos_gain, sin_gain = rope
+        def rotate(n, tables, first, last):
+            cos_gain, sin_gain = tables
+            if first == 0:
+                by_cos = epool.tile([P, TOKEN_TILES, GROUP_HEADS, HEAD], F32, bufs=3)
+                by_sin = epool.tile([P, TOKEN_TILES, GROUP_HEADS, HEAD], F32, bufs=1)
+                straight[n] = by_cos
+                crossed[n] = by_sin
+            tiles = slice(first, last)
+            shape = [P, last - first, GROUP_HEADS, HEAD]
+            half_shape = [P, last - first, GROUP_HEADS, HALF]
             u = u_sb[n]
-            shape = [P, TOKEN_TILES, GROUP_HEADS, HEAD]
-            half_shape = [P, TOKEN_TILES, GROUP_HEADS, HALF]
-            straight = epool.tile(shape, F32, bufs=3)
             nc.vector.tensor_tensor(
-                out=straight[:], in0=u[:], in1=cos_gain[:].unsqueeze(2).to_broadcast(shape), op=ALU.mult
-            )
-            crossed = epool.tile(shape, F32)
-            nc.vector.tensor_tensor(
-                out=crossed[:, :, :, 0:HALF], in0=u[:, :, :, HALF:HEAD],
-                in1=sin_gain[:, :, 0:HALF].unsqueeze(2).to_broadcast(half_shape), op=ALU.mult,
+                out=straight[n][:, tiles, :, :], in0=u[:, tiles, :, :],
+                in1=cos_gain[:, tiles, :].unsqueeze(2).to_broadcast(shape), op=ALU.mult,
             )
             nc.vector.tensor_tensor(
-                out=crossed[:, :, :, HALF:HEAD], in0=u[:, :, :, 0:HALF],
-                in1=sin_gain[:, :, HALF:HEAD].unsqueeze(2).to_broadcast(half_shape), op=ALU.mult,
+                out=crossed[n][:, tiles, :, 0:HALF], in0=u[:, tiles, :, HALF:HEAD],
+                in1=sin_gain[:, tiles, 0:HALF].unsqueeze(2).to_broadcast(half_shape), op=ALU.mult,
             )
-            for i in range(TOKEN_TILES):
+            nc.vector.tensor_tensor(
+                out=crossed[n][:, tiles, :, HALF:HEAD], in0=u[:, tiles, :, 0:HALF],
+                in1=sin_gain[:, tiles, HALF:HEAD].unsqueeze(2).to_broadcast(half_shape), op=ALU.mult,
+            )
+            for i in range(first, last):
                 nc.gpsimd.tensor_tensor(
-                    out=straight[:, i, :, :], in0=straight[:, i, :, :], in1=crossed[:, i, :, :], op=ALU.add
-                )
-            rotated[n] = straight
-
-        def scale_and_store(n):
-            for i in range(TOKEN_TILES):
-                for head in range(GROUP_HEADS):
-                    col = i * GROUP_HEADS + head
-                    nc.scalar.activation(
-                        out=rotated[n][:, i, head, :], in_=rotated[n][:, i, head, :], func=ACT.Copy,
-                        scale=rstd[n][:, col : col + 1],
-                    )
-                nc.sync.dma_start(
-                    out=out_cols[n][i * P : (i + 1) * P, :],
-                    in_=rotated[n][:, i, :, :].rearrange("p a d -> p (a d)"),
+                    out=straight[n][:, i, :, :], in0=straight[n][:, i, :, :], in1=crossed[n][:, i, :, :],
+                    op=ALU.add,
                 )
 
-        def store_plain(n):
-            for i in range(TOKEN_TILES):
-                nc.sync.dma_start(
-                    out=out_cols[n][i * P : (i + 1) * P, :],
-                    in_=u_sb[n][:, i, :, :].rearrange("p a d -> p (a d)"),
-                )
+        def scale_scalar(n, i, head):
+            col = i * GROUP_HEADS + head
+            nc.scalar.activation(
+                out=straight[n][:, i, head, :], in_=straight[n][:, i, head, :], func=ACT.Copy,
+                scale=rstd[n][:, col : col + 1],
+            )
+
+        def scale_gpsimd(n, i, head):
+            col = i * GROUP_HEADS + head
+            nc.gpsimd.tensor_scalar(
+                out=straight[n][:, i, head, :], in0=straight[n][:, i, head, :],
+                scalar1=rstd[n][:, col : col + 1], scalar2=0.0, op0=ALU.mult, op1=ALU.add,
+            )
+
+        def scale_and_store(n, i, scale):
+            for head in range(GROUP_HEADS):
+                scale(n, i, head)
+            nc.sync.dma_start(
+                out=out_cols[n][i * P : (i + 1) * P, :],
+                in_=straight[n][:, i, :, :].rearrange("p a d -> p (a d)"),
+            )
+
+        def store_plain(n, i):
+            nc.sync.dma_start(
+                out=out_cols[n][i * P : (i + 1) * P, :],
+                in_=u_sb[n][:, i, :, :].rearrange("p a d -> p (a d)"),
+            )
 
         for i in range(TOKEN_TILES):
-            x_stats(i)
-        for i in range(TOKEN_TILES):
-            if i >= RUN_AHEAD:
-                x_copy_out(i - RUN_AHEAD)
-            x_scale(i)
-            x_transpose(i)
-        for i in range(TOKEN_TILES - RUN_AHEAD, TOKEN_TILES):
-            x_copy_out(i)
+            x_squares_scalar(i)
+            x_root(i)
+        x_gain(TOKEN_TILES - 1)
+        diagonals_k = diagonals(gain_k, "k")
+        diagonals_q = diagonals(gain_q, "q")
 
-        assert TOKEN_TILES == PASSES
-        for g in range(RUN_AHEAD):
-            transpose_weights(0, g)
-        for step in range(PASSES):
-            copy_out_weights(0, step, (nc.scalar.copy, nc.vector.tensor_copy))
-            if step + RUN_AHEAD < PASSES:
-                transpose_weights(0, step + RUN_AHEAD)
-            x_quantise(step)
-        for g in range(PASSES):
-            quantise_weights(0, g)
+        both_scalar = (nc.scalar.copy, nc.scalar.copy)
+        both_vector = (nc.vector.tensor_copy, nc.vector.tensor_copy)
+        one_each = (nc.scalar.copy, nc.vector.tensor_copy)
 
-        rope = tables_to_psum(tables_q)
-        for g in range(RUN_AHEAD):
-            transpose_weights(1, g)
-        for g in range(PASSES):
-            copy_out_weights(1, g, (nc.scalar.copy, nc.scalar.copy))
-            if g + RUN_AHEAD < PASSES:
-                transpose_weights(1, g + RUN_AHEAD)
-        project(0)
-
-        for n in range(GROUPS):
-            if n + 1 < GROUPS:
-                for g in range(PASSES):
-                    quantise_weights(n + 1, g)
-            for i in range(TOKEN_TILES):
-                add_bias(n, i)
-            if n >= 1:
-                invert_rms(n - 1)
-            if n + 2 < GROUPS:
-                for g in range(RUN_AHEAD):
-                    transpose_weights(n + 2, g)
-            if n == V_GROUP:
-                store_plain(n)
+        def fill_and_empty(unit, copies):
+            kind, part = unit
+            if kind == "h":
+                transpose_h(part)
+                copy_h(part, copies)
             else:
-                head_rms(n)
-            if n + 2 < GROUPS:
-                for g in range(PASSES):
-                    first_copy = nc.vector.tensor_copy if g == 0 else nc.scalar.copy
-                    copy_out_weights(n + 2, g, (first_copy, nc.scalar.copy))
-                    if g + RUN_AHEAD < PASSES:
-                        transpose_weights(n + 2, g + RUN_AHEAD)
-            if n + 1 < GROUPS:
-                project(n + 1)
-            if n >= 1:
-                scale_and_store(n - 1)
-            if n != V_GROUP:
-                rotate(n, rope)
-            if n + 1 == K_GROUP:
-                rope = tables_to_psum(tables_k)
+                transpose_weights(kind, part)
+                copy_weights(kind, part, copies)
+
+        def quantise(unit):
+            kind, part = unit
+            if kind == "h":
+                quantise_h(part)
+            else:
+                quantise_weights(kind, part)
+
+        x_scale(0)
+        x_scale(1)
+        fill_and_empty((0, 0), both_vector)
+        fill_and_empty(("h", 0), both_scalar)
+        fill_and_empty((0, 1), both_scalar)
+        x_scale(2)
+        x_scale_gained(3)
+        fill_and_empty(("h", 1), both_scalar)
+        quantise((0, 0))
+        quantise(("h", 0))
+        fill_and_empty((0, 2), both_scalar)
+        quantise((0, 1))
+        fill_and_empty((0, 3), both_scalar)
+        quantise(("h", 1))
+        fill_and_empty(("h", 2), one_each)
+        quantise((0, 2))
+        turn_cos_sin()
+        fill_and_empty(("h", 3), one_each)
+        quantise((0, 3))
+        fill_and_empty((1, 0), both_scalar)
+        quantise(("h", 2))
+        rope = rope_tables(diagonals_k)
+        fill_and_empty((1, 1), both_scalar)
+        quantise(("h", 3))
+        for i in range(TOKEN_TILES):
+            project(0, i)
+
+        for n in range(V_GROUP):
+            if n == 0:
+                for i in range(TOKEN_TILES):
+                    add_bias(0, i)
+                    if i < 2:
+                        quantise_weights(1, i)
+                    head_squares(0, i)
+                fill_and_empty((1, 2), both_scalar)
+                fill_and_empty((1, 3), both_scalar)
+                head_root(0)
+                quantise_weights(1, 2)
+                quantise_weights(1, 3)
+                for i in range(0, TOKEN_TILES):
+                    rotate(0, rope, i, i + 1)
+            else:
+                for i in range(TOKEN_TILES):
+                    add_bias(n, i)
+                invert_rms(n - 1)
+            for g in range(PASSES):
+                if n + 2 < GROUPS:
+                    fill_and_empty((n + 2, g), both_scalar)
+                if n > 0:
+                    quantise_weights(n + 1, g)
+                if n == LAST_ROPE_GROUP and g == 0:
+                    for i in range(TOKEN_TILES):
+                        head_squares(n, i)
+                    head_root(n)
+                if n > 0 and g == 0:
+                    for i in range(TOKEN_TILES):
+                        scale_and_store(n - 1, i, scale_scalar if i in SCALAR_TILES else scale_gpsimd)
+            for i in range(TOKEN_TILES):
+                project(n + 1, i)
+            if n == 0:
+                rope = rope_tables(diagonals_q)
+            if 0 < n < LAST_ROPE_GROUP:
+                for i in range(TOKEN_TILES):
+                    head_squares(n, i)
+                head_root(n)
+            if 0 < n < LAST_ROPE_GROUP:
+                for i in range(TOKEN_TILES):
+                    rotate(n, rope, i, i + 1)
+
+        for i in range(TOKEN_TILES):
+            rotate(LAST_ROPE_GROUP, rope, i, i + 1)
+            if i == 0:
+                invert_rms(LAST_ROPE_GROUP)
+            scale_and_store(LAST_ROPE_GROUP, i, scale_scalar)
+            add_bias(V_GROUP, i)
+            store_plain(V_GROUP, i)

@@ -41,7 +41,12 @@ RUN_AHEAD = RING_BANKS // UNIT_BANKS
 BANK_PASSES = PASSES // UNIT_BANKS
 BANK_ROW_TILES = ROW_TILES // UNIT_BANKS
 BANK_BF16 = 1024
+
+ROW_GAIN_K = HID
+ROW_GAIN_Q = ROW_GAIN_K + HEAD
+ROW_LENGTH = ROW_GAIN_Q + HEAD
 ROTATE_TILES = 2
+HALF_TILES = TOKEN_TILES // 2
 SCALAR_TILES = (0, 1, 2)
 
 FLOPS = 2 * TOKENS * HID * GROUPS * GROUP
@@ -52,14 +57,13 @@ def tile_qwen2decoderlayer_pa_kernel(
 ):
     nc = tc.nc
 
-    q_flat = out_0.rearrange("m a d -> m (a d)")
+    q_flat = out_0.rearrange("(p i) a d -> p i (a d)", i=TOKEN_TILES)
     q_slices = [slice(n * GROUP, (n + 1) * GROUP) for n in range(Q_GROUPS)]
     weight_rows = [wk] + [wq[cols, :] for cols in q_slices] + [wv]
-    bias_rows = [bk] + [bq[cols] for cols in q_slices] + [bv]
     out_cols = (
-        [out_1.rearrange("m a d -> m (a d)")]
-        + [q_flat[:, cols] for cols in q_slices]
-        + [out_2.rearrange("m a d -> m (a d)")]
+        [out_1.rearrange("(p i) a d -> p i (a d)", i=TOKEN_TILES)]
+        + [q_flat[:, :, cols] for cols in q_slices]
+        + [out_2.rearrange("(p i) a d -> p i (a d)", i=TOKEN_TILES)]
     )
 
     with ExitStack() as ctx:
@@ -75,13 +79,19 @@ def tile_qwen2decoderlayer_pa_kernel(
         table_psum = ctx.enter_context(tc.psum_pool(name="table_psum", bufs=1))
 
         x_sb = const.tile([P, TOKEN_TILES, HID], BF16)
-        nc.sync.dma_start(out=x_sb[:, 0, :], in_=x[0:P, :])
-        lnw_row = const.tile([P, HID], BF16)
-        nc.vector.memset(lnw_row[:].bitcast(I32), 0)
-        nc.sync.dma_start(out=lnw_row[0:1, :], in_=ln1_w.unsqueeze(0))
-        nc.sync.dma_start(out=x_sb[:, 1, :], in_=x[P : 2 * P, :])
+        x_rows = x.rearrange("(p i) k -> p i k", i=TOKEN_TILES)
+        nc.sync.dma_start(out=x_sb[:, 0, :], in_=x_rows[:, 0, :])
+        row = const.tile([P, ROW_LENGTH], BF16)
+        nc.vector.memset(row[:].bitcast(I32), 0)
 
-        bias = const.tile([P, GROUPS * GROUP], BF16)
+        def load_row(first, vector):
+            nc.sync.dma_start(out=row[0:1, first : first + vector.shape[0]], in_=vector.unsqueeze(0))
+
+        load_row(0, ln1_w)
+        load_row(ROW_GAIN_K, k_norm_w)
+        load_row(ROW_GAIN_Q, q_norm_w)
+        nc.sync.dma_start(out=x_sb[:, 1, :], in_=x_rows[:, 1, :])
+
         w_sb = {}
 
         def load_columns(n, first, last):
@@ -90,33 +100,27 @@ def tile_qwen2decoderlayer_pa_kernel(
                 in_=weight_rows[n].rearrange("(r p) k -> p r k", p=P)[:, :, first:last],
             )
 
-        def load_bias(n):
-            nc.sync.dma_start(
-                out=bias[:, n * GROUP : (n + 1) * GROUP], in_=bias_rows[n].partition_broadcast(P)
-            )
-
         def load_weights(n):
             w_rows = wpool.tile([P, ROW_TILES, HID], BF16)
             w_sb[n] = w_rows
             load_columns(n, 0, HID)
-            load_bias(n)
 
         w_rows = wpool.tile([P, ROW_TILES, HID], BF16)
         w_sb[0] = w_rows
         load_columns(0, 0, HID // 2)
         for i in range(2, TOKEN_TILES):
-            nc.sync.dma_start(out=x_sb[:, i, :], in_=x[i * P : (i + 1) * P, :])
+            nc.sync.dma_start(out=x_sb[:, i, :], in_=x_rows[:, i, :])
         load_columns(0, HID // 2, HID)
         cos_sin = const.tile([P, 2, TOKEN_TILES, HEAD], BF16)
-        nc.sync.dma_start(out=cos_sin[:, 0, :, :], in_=cos.rearrange("(i p) d -> p i d", p=P))
-        nc.sync.dma_start(out=cos_sin[:, 1, :, :], in_=sin.rearrange("(i p) d -> p i d", p=P))
-        gain_k = const.tile([P, HEAD], BF16)
-        nc.sync.dma_start(out=gain_k[:], in_=k_norm_w.partition_broadcast(P))
-        gain_q = const.tile([P, HEAD], BF16)
-        nc.sync.dma_start(out=gain_q[:], in_=q_norm_w.partition_broadcast(P))
-        load_bias(0)
-        for n in range(1, WEIGHT_BUFS):
-            load_weights(n)
+        nc.sync.dma_start(out=cos_sin[:, 0, :, :], in_=cos.rearrange("(p i) d -> p i d", i=TOKEN_TILES))
+        nc.sync.dma_start(out=cos_sin[:, 1, :, :], in_=sin.rearrange("(p i) d -> p i d", i=TOKEN_TILES))
+        bias = const.tile([P, GROUPS * GROUP], BF16)
+        load_weights(1)
+        nc.sync.dma_start(out=bias[:, 0:GROUP], in_=bk.partition_broadcast(P))
+        load_weights(2)
+        nc.sync.dma_start(out=bias[:, GROUP : V_GROUP * GROUP], in_=bq.partition_broadcast(P))
+        load_weights(3)
+        nc.sync.dma_start(out=bias[:, V_GROUP * GROUP :], in_=bv.partition_broadcast(P))
 
         ident_f = const.tile([P, P], F32)
         make_identity(nc, ident_f[:])
@@ -130,16 +134,28 @@ def tile_qwen2decoderlayer_pa_kernel(
 
         ones = const.tile([P, P], BF16)
         nc.vector.memset(ones[:], 1.0)
+
+        def spread(bank, first, width):
+            for part in range(0, width, GROUP):
+                end = min(part + GROUP, width)
+                nc.tensor.matmul(
+                    out=bank[:, part:end], lhsT=ones[:], rhs=row[:, first + part : first + end],
+                    start=True, stop=True,
+                )
+
         lnw_banks = []
         for half in range(UNIT_BANKS):
             bank = table_psum.tile([P, BANK_BF16], BF16, tag="table%d" % half, name="lnw_bank")
-            for first in range(0, BANK_BF16, GROUP):
-                nc.tensor.matmul(
-                    out=bank[:, first : first + GROUP], lhsT=ones[:],
-                    rhs=lnw_row[:, half * BANK_BF16 + first : half * BANK_BF16 + first + GROUP],
-                    start=True, stop=True,
-                )
+            spread(bank, half * BANK_BF16, BANK_BF16)
             lnw_banks.append(bank)
+
+        gains = const.tile([P, 2 * HEAD], BF16)
+        gain_k = gains[:, 0:HEAD]
+        gain_q = gains[:, HEAD : 2 * HEAD]
+        bank = ring.tile([P, BANK_BF16], BF16, tag="bank")
+        spread(bank, ROW_GAIN_K, 2 * HEAD)
+        nc.vector.tensor_copy(out=gains[:], in_=bank[:, 0 : 2 * HEAD])
+
         h_codes = const.tile([P, TOKEN_TILES, PASSES, P], U32, align_bytes=64)
         h_scales = const.tile([P, TOKEN_TILES, PASSES, P], U8, align_bytes=64)
         x_ss = const.tile([P, TOKEN_TILES], F32)
@@ -170,9 +186,9 @@ def tile_qwen2decoderlayer_pa_kernel(
         def x_gain(i):
             for half in range(UNIT_BANKS):
                 nc.vector.tensor_copy(
-                    out=lnw_row[:, half * BANK_BF16 : (half + 1) * BANK_BF16], in_=lnw_banks[half][:]
+                    out=row[:, half * BANK_BF16 : (half + 1) * BANK_BF16], in_=lnw_banks[half][:]
                 )
-            nc.gpsimd.tensor_tensor(out=x_gained[:], in0=x_sb[:, i, :], in1=lnw_row[:], op=ALU.mult)
+            nc.gpsimd.tensor_tensor(out=x_gained[:], in0=x_sb[:, i, :], in1=row[:, 0:HID], op=ALU.mult)
 
         def word_order(row):
             return row.rearrange("p (g j u e) -> p u g j e", j=P, u=WORDS, e=PAIR)
@@ -239,7 +255,7 @@ def tile_qwen2decoderlayer_pa_kernel(
                 op0=ALU.mult, op1=ALU.add,
             )
             pair = const.tile([P, 2, HEAD], BF16, name="diagonals_" + name)
-            nc.gpsimd.tensor_tensor(out=pair[:, 0, :], in0=ident_bf[:], in1=gain[:], op=ALU.mult)
+            nc.gpsimd.tensor_tensor(out=pair[:, 0, :], in0=ident_bf[:], in1=gain, op=ALU.mult)
             nc.gpsimd.tensor_tensor(out=pair[:, 1, :], in0=ident_bf[:], in1=swapped[:], op=ALU.mult)
             return pair
 
@@ -403,20 +419,19 @@ def tile_qwen2decoderlayer_pa_kernel(
             for head in range(GROUP_HEADS):
                 scale(n, i, head)
             nc.sync.dma_start(
-                out=out_cols[n][i * P : (i + 1) * P, :],
+                out=out_cols[n][:, i, :],
                 in_=straight[n][:, i, :, :].rearrange("p a d -> p (a d)"),
             )
 
         def store_plain(n, i):
             nc.sync.dma_start(
-                out=out_cols[n][i * P : (i + 1) * P, :],
+                out=out_cols[n][:, i, :],
                 in_=u_sb[n][:, i, :, :].rearrange("p a d -> p (a d)"),
             )
 
         for i in range(TOKEN_TILES):
             x_squares_scalar(i)
             x_root(i)
-        x_gain(TOKEN_TILES - 1)
         diagonals_k = diagonals(gain_k, "k")
         diagonals_q = diagonals(gain_q, "q")
 
@@ -441,6 +456,7 @@ def tile_qwen2decoderlayer_pa_kernel(
                 quantise_weights(kind, part)
 
         x_scale(0)
+        x_gain(TOKEN_TILES - 1)
         x_scale(1)
         fill_and_empty((0, 0), both_vector)
         fill_and_empty(("h", 0), both_scalar)

@@ -32,7 +32,7 @@ Q_GROUPS = 4
 GROUPS = Q_GROUPS + 2
 K_GROUP = 0
 V_GROUP = GROUPS - 1
-LAST_ROPE_GROUP = V_GROUP - 1
+LAST = V_GROUP - 1
 
 WEIGHT_BUFS = 4
 RING_BANKS = 6
@@ -152,43 +152,42 @@ def tile_qwen2decoderlayer_pa_kernel(
         gains = const.tile([P, 2 * HEAD], BF16)
         gain_k = gains[:, 0:HEAD]
         gain_q = gains[:, HEAD : 2 * HEAD]
-        bank = ring.tile([P, BANK_BF16], BF16, tag="bank")
-        spread(bank, ROW_GAIN_K, 2 * HEAD)
-        nc.vector.tensor_copy(out=gains[:], in_=bank[:, 0 : 2 * HEAD])
+
+        def spread_gains():
+            bank = ring.tile([P, BANK_BF16], BF16, tag="bank")
+            spread(bank, ROW_GAIN_K, 2 * HEAD)
+            nc.vector.tensor_copy(out=gains[:], in_=bank[:, 0 : 2 * HEAD])
 
         h_codes = const.tile([P, TOKEN_TILES, PASSES, P], U32, align_bytes=64)
         h_scales = const.tile([P, TOKEN_TILES, PASSES, P], U8, align_bytes=64)
         x_ss = const.tile([P, TOKEN_TILES], F32)
         x_rms = const.tile([P, TOKEN_TILES], F32)
         x_rstd = const.tile([P, TOKEN_TILES], F32)
-        x_gained = const.tile([P, HID], F32)
+        rest = const.tile([P, 1], F32)
+        squares_v = const.tile([P, HID // 2], BF16)
         h_tiles = {}
         banks = {}
         grouped = {}
 
-        def x_squares_scalar(i):
+        def x_squares(i):
+            end = HID // 2 if i == 0 else HID
             nc.scalar.activation(
-                out=squares[:], in_=x_sb[:, i, :], func=ACT.Square, accum_out=x_ss[:, i : i + 1]
+                out=squares[:, 0:end], in_=x_sb[:, i, 0:end], func=ACT.Square, accum_out=x_ss[:, i : i + 1]
             )
-
-        def x_squares_vector(i):
-            nc.vector.scalar_tensor_tensor(
-                out=x_gained[:].bitcast(BF16)[:, 0:HID], in0=x_sb[:, i, :], scalar=1.0, in1=x_sb[:, i, :],
-                op0=ALU.mult, op1=ALU.mult, accum_out=x_ss[:, i : i + 1],
-            )
+            if i == 0:
+                nc.vector.scalar_tensor_tensor(
+                    out=squares_v[:], in0=x_sb[:, i, end:HID], scalar=1.0, in1=x_sb[:, i, end:HID],
+                    op0=ALU.mult, op1=ALU.mult, accum_out=rest[:],
+                )
+                nc.vector.tensor_scalar(
+                    out=rest[:], in0=rest[:], scalar1=1.0 / HID, scalar2=EPS, op0=ALU.mult, op1=ALU.add
+                )
 
         def x_root(i):
             nc.scalar.activation(
                 out=x_rms[:, i : i + 1], in_=x_ss[:, i : i + 1], func=ACT.Sqrt,
-                scale=1.0 / HID, bias=eps[:, 0:1],
+                scale=1.0 / HID, bias=rest[:] if i == 0 else eps[:],
             )
-
-        def x_gain(i):
-            for half in range(UNIT_BANKS):
-                nc.vector.tensor_copy(
-                    out=row[:, half * BANK_BF16 : (half + 1) * BANK_BF16], in_=lnw_banks[half][:]
-                )
-            nc.gpsimd.tensor_tensor(out=x_gained[:], in0=x_sb[:, i, :], in1=row[:, 0:HID], op=ALU.mult)
 
         def word_order(row):
             return row.rearrange("p (g j u e) -> p u g j e", j=P, u=WORDS, e=PAIR)
@@ -205,16 +204,6 @@ def tile_qwen2decoderlayer_pa_kernel(
                         in0=x_words[:, u, :, :, :], scalar=x_rstd[:, i : i + 1],
                         in1=lnw_words[:, u, :, :, :], op0=ALU.mult, op1=ALU.mult,
                     )
-            h_tiles[i] = h_tile
-
-        def x_scale_gained(i):
-            nc.vector.reciprocal(out=x_rstd[:, i : i + 1], in_=x_rms[:, i : i + 1])
-            h_tile = hpool.tile([P, PASSES, WORDS, P, PAIR], BF16)
-            gained_words = word_order(x_gained[:])
-            for u in range(WORDS):
-                nc.vector.tensor_scalar_mul(
-                    h_tile[:, :, u, :, :], gained_words[:, u, :, :, :], x_rstd[:, i : i + 1]
-                )
             h_tiles[i] = h_tile
 
         def transpose_h(i):
@@ -362,15 +351,21 @@ def tile_qwen2decoderlayer_pa_kernel(
                     func=ACT.Square, accum_out=ss[n][:, col : col + 1],
                 )
 
-        def head_root(n):
-            rms = stats.tile([P, TOKEN_TILES * GROUP_HEADS], F32)
-            nc.scalar.activation(out=rms[:], in_=ss[n][:], func=ACT.Sqrt, scale=1.0 / HEAD, bias=eps[:, 0:1])
-            rms_sb[n] = rms
+        def head_root(n, first, last):
+            cols = slice(first * GROUP_HEADS, last * GROUP_HEADS)
+            if first == 0:
+                rms = stats.tile([P, TOKEN_TILES * GROUP_HEADS], F32)
+                rms_sb[n] = rms
+            nc.scalar.activation(
+                out=rms_sb[n][:, cols], in_=ss[n][:, cols], func=ACT.Sqrt, scale=1.0 / HEAD, bias=eps[:, 0:1]
+            )
 
-        def invert_rms(n):
-            inv = stats.tile([P, TOKEN_TILES * GROUP_HEADS], F32)
-            nc.vector.reciprocal(out=inv[:], in_=rms_sb[n][:])
-            rstd[n] = inv
+        def invert_rms(n, first, last):
+            cols = slice(first * GROUP_HEADS, last * GROUP_HEADS)
+            if first == 0:
+                inv = stats.tile([P, TOKEN_TILES * GROUP_HEADS], F32)
+                rstd[n] = inv
+            nc.vector.reciprocal(out=rstd[n][:, cols], in_=rms_sb[n][:, cols])
 
         def rotate(n, tables, first, last):
             cos_gain, sin_gain = tables
@@ -430,8 +425,9 @@ def tile_qwen2decoderlayer_pa_kernel(
             )
 
         for i in range(TOKEN_TILES):
-            x_squares_scalar(i)
+            x_squares(i)
             x_root(i)
+        spread_gains()
         diagonals_k = diagonals(gain_k, "k")
         diagonals_q = diagonals(gain_q, "q")
 
@@ -456,13 +452,12 @@ def tile_qwen2decoderlayer_pa_kernel(
                 quantise_weights(kind, part)
 
         x_scale(0)
-        x_gain(TOKEN_TILES - 1)
         x_scale(1)
         fill_and_empty((0, 0), both_vector)
         fill_and_empty(("h", 0), both_scalar)
         fill_and_empty((0, 1), both_scalar)
         x_scale(2)
-        x_scale_gained(3)
+        x_scale(3)
         fill_and_empty(("h", 1), both_scalar)
         quantise((0, 0))
         quantise(("h", 0))
@@ -480,55 +475,56 @@ def tile_qwen2decoderlayer_pa_kernel(
         rope = rope_tables(diagonals_k)
         fill_and_empty((1, 1), both_scalar)
         quantise(("h", 3))
-        for i in range(TOKEN_TILES):
+        for i in range(HALF_TILES):
             project(0, i)
 
         for n in range(V_GROUP):
-            if n == 0:
-                for i in range(TOKEN_TILES):
-                    add_bias(0, i)
-                    if i < 2:
-                        quantise_weights(1, i)
-                    head_squares(0, i)
-                fill_and_empty((1, 2), both_scalar)
-                fill_and_empty((1, 3), both_scalar)
-                head_root(0)
-                quantise_weights(1, 2)
-                quantise_weights(1, 3)
-                for i in range(0, TOKEN_TILES):
-                    rotate(0, rope, i, i + 1)
-            else:
-                for i in range(TOKEN_TILES):
+            for half in range(2):
+                tiles = range(half * HALF_TILES, (half + 1) * HALF_TILES)
+                others = range((1 - half) * HALF_TILES, (2 - half) * HALF_TILES)
+                for i in tiles:
                     add_bias(n, i)
-                invert_rms(n - 1)
-            for g in range(PASSES):
-                if n + 2 < GROUPS:
-                    fill_and_empty((n + 2, g), both_scalar)
-                if n > 0:
-                    quantise_weights(n + 1, g)
-                if n == LAST_ROPE_GROUP and g == 0:
-                    for i in range(TOKEN_TILES):
-                        head_squares(n, i)
-                    head_root(n)
-                if n > 0 and g == 0:
+                if half == 0 and n > 0:
+                    invert_rms(n - 1, 0, TOKEN_TILES)
+                ahead = n + 1 + half
+                if ahead < GROUPS:
+                    for g in others:
+                        fill_and_empty((ahead, g), both_scalar)
+                if half == 0:
+                    for g in range(PASSES):
+                        quantise_weights(n + 1, g)
+                for i in others:
+                    project(n + half, i)
+                for i in tiles:
+                    head_squares(n, i)
+                if half == 1 and n < LAST:
+                    head_root(n, 0, TOKEN_TILES)
+                if n == LAST:
+                    head_root(n, half * HALF_TILES, (half + 1) * HALF_TILES)
+                if n > 0 and half == 0:
                     for i in range(TOKEN_TILES):
                         scale_and_store(n - 1, i, scale_scalar if i in SCALAR_TILES else scale_gpsimd)
-            for i in range(TOKEN_TILES):
-                project(n + 1, i)
+                if n < LAST or half == 0:
+                    for i in tiles:
+                        rotate(n, rope, i, i + 1)
+                if n == LAST and half == 0:
+                    invert_rms(n, 0, HALF_TILES)
+                    for i in tiles:
+                        scale_and_store(n, i, scale_scalar)
             if n == 0:
                 rope = rope_tables(diagonals_q)
-            if 0 < n < LAST_ROPE_GROUP:
-                for i in range(TOKEN_TILES):
-                    head_squares(n, i)
-                head_root(n)
-            if 0 < n < LAST_ROPE_GROUP:
-                for i in range(TOKEN_TILES):
-                    rotate(n, rope, i, i + 1)
 
-        for i in range(TOKEN_TILES):
-            rotate(LAST_ROPE_GROUP, rope, i, i + 1)
-            if i == 0:
-                invert_rms(LAST_ROPE_GROUP)
-            scale_and_store(LAST_ROPE_GROUP, i, scale_scalar)
+        for i in range(HALF_TILES, TOKEN_TILES):
+            project(V_GROUP, i)
+        add_bias(V_GROUP, 0)
+        store_plain(V_GROUP, 0)
+        rotate(LAST, rope, 2, 3)
+        add_bias(V_GROUP, 1)
+        store_plain(V_GROUP, 1)
+        rotate(LAST, rope, 3, 4)
+        invert_rms(LAST, HALF_TILES, TOKEN_TILES)
+        for i in range(HALF_TILES, TOKEN_TILES):
+            scale_and_store(LAST, i, scale_scalar)
+        for i in range(HALF_TILES, TOKEN_TILES):
             add_bias(V_GROUP, i)
             store_plain(V_GROUP, i)

@@ -24,6 +24,7 @@ PACK = 4
 K_PASS = P * PACK
 PASSES = HID // K_PASS
 PAIR = 2
+PASS_WORDS = K_PASS // PAIR
 WORDS = PACK // PAIR
 GROUP = 512
 GROUP_HEADS = GROUP // HEAD
@@ -47,7 +48,7 @@ ROW_GAIN_Q = ROW_GAIN_K + HEAD
 ROW_LENGTH = ROW_GAIN_Q + HEAD
 ROTATE_TILES = 2
 HALF_TILES = TOKEN_TILES // 2
-SCALAR_TILES = (0, 1, 2)
+SCALAR_TILES = (0, 1, 2, 3)
 
 FLOPS = 2 * TOKENS * HID * GROUPS * GROUP
 
@@ -70,7 +71,7 @@ def tile_qwen2decoderlayer_pa_kernel(
         ctx.enter_context(tc.manual_schedule())
         const = ctx.enter_context(tc.tile_pool(name="const", bufs=1))
         hpool = ctx.enter_context(tc.tile_pool(name="hpool", bufs=TOKEN_TILES))
-        wpool = ctx.enter_context(tc.tile_pool(name="wpool", bufs=WEIGHT_BUFS))
+        wpool = ctx.enter_context(tc.tile_pool(name="wpool", bufs=2 * WEIGHT_BUFS))
         gpool = ctx.enter_context(tc.tile_pool(name="gpool", bufs=6))
         cpool = ctx.enter_context(tc.tile_pool(name="cpool", bufs=2))
         epool = ctx.enter_context(tc.tile_pool(name="epool", bufs=2))
@@ -94,23 +95,37 @@ def tile_qwen2decoderlayer_pa_kernel(
 
         w_sb = {}
 
-        def load_columns(n, first, last):
-            nc.sync.dma_start(
-                out=w_sb[n][:, :, first:last],
-                in_=weight_rows[n].rearrange("(r p) k -> p r k", p=P)[:, :, first:last],
-            )
-
         def load_weights(n):
-            w_rows = wpool.tile([P, ROW_TILES, HID], BF16)
-            w_sb[n] = w_rows
-            load_columns(n, 0, HID)
+            halves = []
+            for half in range(2):
+                rows = slice(half * GROUP // 2, (half + 1) * GROUP // 2)
+                w_half = wpool.tile([P, ROW_TILES // 2, HID], BF16, tag="w_half")
+                nc.sync.dma_start(out=w_half[:], in_=weight_rows[n][rows, :].rearrange("(r p) k -> p r k", p=P))
+                halves.append(w_half)
+            w_sb[n] = halves
 
-        w_rows = wpool.tile([P, ROW_TILES, HID], BF16)
-        w_sb[0] = w_rows
-        load_columns(0, 0, HID // 2)
+        def load_features(n, half):
+            w_half = wpool.tile([P, ROW_TILES, HID // 2], BF16, tag="w_half")
+            nc.sync.dma_start(
+                out=w_half[:],
+                in_=weight_rows[n][:, half * HID // 2 : (half + 1) * HID // 2].rearrange("(r p) k -> p r k", p=P),
+            )
+            w_sb.setdefault(n, []).append(w_half)
+
+        def weight_words(n, r, g):
+            if n == 0:
+                half, part = divmod(g, PASSES // 2)
+                words = w_sb[n][half][:, r, :].bitcast(F32)
+            else:
+                half, r = divmod(r, ROW_TILES // 2)
+                part = g
+                words = w_sb[n][half][:, r, :].bitcast(F32)
+            return words[:, part * PASS_WORDS : (part + 1) * PASS_WORDS]
+
+        load_features(0, 0)
         for i in range(2, TOKEN_TILES):
             nc.sync.dma_start(out=x_sb[:, i, :], in_=x_rows[:, i, :])
-        load_columns(0, HID // 2, HID)
+        load_features(0, 1)
         cos_sin = const.tile([P, 2, TOKEN_TILES, HEAD], BF16)
         nc.sync.dma_start(out=cos_sin[:, 0, :, :], in_=cos.rearrange("(p i) d -> p i d", i=TOKEN_TILES))
         nc.sync.dma_start(out=cos_sin[:, 1, :, :], in_=sin.rearrange("(p i) d -> p i d", i=TOKEN_TILES))
@@ -257,10 +272,15 @@ def tile_qwen2decoderlayer_pa_kernel(
                     nc.tensor.transpose(bank[:, half, i, :], cos_sin[:, half, i, :], ident_bf[:])
             nc.scalar.copy(out=turned[:], in_=bank[:])
 
-        def rope_tables(pair):
+        def rope_tables(pair, warm=0):
             in_psum = []
             for half in range(2):
                 bank = table_psum.tile([P, TOKEN_TILES, HEAD], F32, tag="table%d" % half, name="rope_bank")
+                for part in range(warm):
+                    nc.tensor.matmul(
+                        out=bank[:].rearrange("p i d -> p (i d)"), lhsT=ones[:], rhs=row[:, 0:GROUP],
+                        start=True, stop=True,
+                    )
                 for i in range(TOKEN_TILES):
                     nc.tensor.matmul(
                         out=bank[:, i, :], lhsT=turned[:, half, i, :], rhs=pair[:, half, :],
@@ -284,12 +304,9 @@ def tile_qwen2decoderlayer_pa_kernel(
                 w_t = ring.tile([P, WORDS, BANK_ROW_TILES * P], F32, tag="bank")
                 for u in range(WORDS):
                     for rr in range(BANK_ROW_TILES):
-                        first = (K_PASS // PAIR) * g + u
-                        last = (K_PASS // PAIR) * (g + 1)
+                        words = weight_words(n, BANK_ROW_TILES * rp + rr, g)
                         nc.tensor.transpose(
-                            w_t[:, u, rr * P : (rr + 1) * P],
-                            w_sb[n][:, BANK_ROW_TILES * rp + rr, :].bitcast(F32)[:, first:last:WORDS],
-                            ident_f[:],
+                            w_t[:, u, rr * P : (rr + 1) * P], words[:, u:PASS_WORDS:WORDS], ident_f[:]
                         )
                 banks[(n, g, rp)] = w_t
             if g == PASSES - 1 and n + WEIGHT_BUFS < GROUPS:
@@ -473,58 +490,44 @@ def tile_qwen2decoderlayer_pa_kernel(
         fill_and_empty((1, 0), both_scalar)
         quantise(("h", 2))
         rope = rope_tables(diagonals_k)
-        fill_and_empty((1, 1), both_scalar)
         quantise(("h", 3))
-        for i in range(HALF_TILES):
-            project(0, i)
+        quantise((1, 0))
 
-        for n in range(V_GROUP):
-            for half in range(2):
-                tiles = range(half * HALF_TILES, (half + 1) * HALF_TILES)
-                others = range((1 - half) * HALF_TILES, (2 - half) * HALF_TILES)
-                for i in tiles:
-                    add_bias(n, i)
-                if half == 0 and n > 0:
-                    invert_rms(n - 1, 0, TOKEN_TILES)
-                ahead = n + 1 + half
-                if ahead < GROUPS:
-                    for g in others:
-                        fill_and_empty((ahead, g), both_scalar)
-                if half == 0:
-                    for g in range(PASSES):
-                        quantise_weights(n + 1, g)
-                for i in others:
-                    project(n + half, i)
-                for i in tiles:
-                    head_squares(n, i)
-                if half == 1 and n < LAST:
-                    head_root(n, 0, TOKEN_TILES)
-                if n == LAST:
-                    head_root(n, half * HALF_TILES, (half + 1) * HALF_TILES)
-                if n > 0 and half == 0:
-                    for i in range(TOKEN_TILES):
-                        scale_and_store(n - 1, i, scale_scalar if i in SCALAR_TILES else scale_gpsimd)
-                if n < LAST or half == 0:
-                    for i in tiles:
-                        rotate(n, rope, i, i + 1)
-                if n == LAST and half == 0:
-                    invert_rms(n, 0, HALF_TILES)
-                    for i in tiles:
-                        scale_and_store(n, i, scale_scalar)
-            if n == 0:
-                rope = rope_tables(diagonals_q)
+        units = [(n, i) for n in range(GROUPS) for i in range(TOKEN_TILES)]
 
-        for i in range(HALF_TILES, TOKEN_TILES):
-            project(V_GROUP, i)
-        add_bias(V_GROUP, 0)
-        store_plain(V_GROUP, 0)
-        rotate(LAST, rope, 2, 3)
-        add_bias(V_GROUP, 1)
-        store_plain(V_GROUP, 1)
-        rotate(LAST, rope, 3, 4)
-        invert_rms(LAST, HALF_TILES, TOKEN_TILES)
-        for i in range(HALF_TILES, TOKEN_TILES):
-            scale_and_store(LAST, i, scale_scalar)
-        for i in range(HALF_TILES, TOKEN_TILES):
-            add_bias(V_GROUP, i)
-            store_plain(V_GROUP, i)
+        def at(beat):
+            return units[beat] if 0 <= beat < len(units) else (GROUPS, 0)
+
+        def finish(n, i):
+            scale_and_store(n, i, scale_scalar if i in SCALAR_TILES or n == LAST else scale_gpsimd)
+
+        finish_at = {5:[[0,0]],6:[[0,1]],7:[[0,2]],8:[[0,3]],9:[[1,0]],10:[[1,1]],11:[[1,2]],12:[[1,3]],13:[[2,0]],14:[[2,1]],15:[[2,2]],16:[[2,3]],17:[[3,0]],18:[[3,1]],19:[[3,2],[3,3]],20:[[4,0],[4,1]],21:[[4,2],[4,3]]}
+        for beat in range(len(units)):
+            unit = at(beat + PASSES + 1)
+            n, i = at(beat)
+            last, tile = at(beat - 1) if beat > 0 else (GROUPS, 0)
+            if unit[0] < GROUPS:
+                fill_and_empty(unit, both_scalar)
+            project(n, i)
+            if beat == PASSES + 1:
+                rope_q = rope_tables(diagonals_q)
+            add_bias(n, i)
+            if n == V_GROUP:
+                store_plain(n, i)
+            if last < V_GROUP:
+                rotate(last, rope if last == K_GROUP else rope_q, tile, tile + 1)
+            if unit[0] < GROUPS:
+                quantise(unit)
+            if beat == 19:
+                invert_rms(LAST, 0, HALF_TILES)
+            if beat == 21:
+                invert_rms(LAST, HALF_TILES, TOKEN_TILES)
+            if last < V_GROUP:
+                head_squares(last, tile)
+                if last < LAST and tile == TOKEN_TILES - 1:
+                    head_root(last, 0, TOKEN_TILES)
+                    invert_rms(last, 0, TOKEN_TILES)
+                if last == LAST and tile % HALF_TILES == 1:
+                    head_root(last, tile - 1, tile + 1)
+            for done, j in finish_at.get(beat, []):
+                finish(done, j)

@@ -48,7 +48,6 @@ ROW_GAIN_Q = ROW_GAIN_K + HEAD
 ROW_LENGTH = ROW_GAIN_Q + HEAD
 ROTATE_TILES = 2
 HALF_TILES = TOKEN_TILES // 2
-SCALAR_TILES = (0, 1, 2, 3)
 
 FLOPS = 2 * TOKENS * HID * GROUPS * GROUP
 
@@ -299,9 +298,14 @@ def tile_qwen2decoderlayer_pa_kernel(
         rms_sb = {}
         rstd = {}
 
-        def transpose_weights(n, g):
+        def transpose_weights(n, g, warm=0):
             for rp in range(UNIT_BANKS):
                 w_t = ring.tile([P, WORDS, BANK_ROW_TILES * P], F32, tag="bank")
+                for part in range(warm if rp == 0 else 0):
+                    nc.tensor.matmul(
+                        out=w_t[:].rearrange("p u f -> p (u f)"), lhsT=ones[:], rhs=row[:, 0:GROUP],
+                        start=True, stop=True,
+                    )
                 for u in range(WORDS):
                     for rr in range(BANK_ROW_TILES):
                         words = weight_words(n, BANK_ROW_TILES * rp + rr, g)
@@ -427,8 +431,9 @@ def tile_qwen2decoderlayer_pa_kernel(
                 scalar1=rstd[n][:, col : col + 1], scalar2=0.0, op0=ALU.mult, op1=ALU.add,
             )
 
-        def scale_and_store(n, i, scale):
+        def scale_and_store(n, i, gpsimd_heads):
             for head in range(GROUP_HEADS):
+                scale = scale_gpsimd if head in gpsimd_heads else scale_scalar
                 scale(n, i, head)
             nc.sync.dma_start(
                 out=out_cols[n][:, i, :],
@@ -441,24 +446,17 @@ def tile_qwen2decoderlayer_pa_kernel(
                 in_=u_sb[n][:, i, :, :].rearrange("p a d -> p (a d)"),
             )
 
-        for i in range(TOKEN_TILES):
-            x_squares(i)
-            x_root(i)
-        spread_gains()
-        diagonals_k = diagonals(gain_k, "k")
-        diagonals_q = diagonals(gain_q, "q")
-
         both_scalar = (nc.scalar.copy, nc.scalar.copy)
         both_vector = (nc.vector.tensor_copy, nc.vector.tensor_copy)
         one_each = (nc.scalar.copy, nc.vector.tensor_copy)
 
-        def fill_and_empty(unit, copies):
+        def fill_and_empty(unit, copies, warm=0):
             kind, part = unit
             if kind == "h":
                 transpose_h(part)
                 copy_h(part, copies)
             else:
-                transpose_weights(kind, part)
+                transpose_weights(kind, part, warm)
                 copy_weights(kind, part, copies)
 
         def quantise(unit):
@@ -468,6 +466,22 @@ def tile_qwen2decoderlayer_pa_kernel(
             else:
                 quantise_weights(kind, part)
 
+        units = [(n, i) for n in range(GROUPS) for i in range(TOKEN_TILES)]
+
+        def at(beat):
+            return units[beat] if 0 <= beat < len(units) else (GROUPS, 0)
+
+        x_squares(0)
+        x_root(0)
+        x_squares(1)
+        x_root(1)
+        x_squares(2)
+        x_root(2)
+        x_squares(3)
+        x_root(3)
+        spread_gains()
+        diagonals_k = diagonals(gain_k, "k")
+        diagonals_q = diagonals(gain_q, "q")
         x_scale(0)
         x_scale(1)
         fill_and_empty((0, 0), both_vector)
@@ -489,23 +503,15 @@ def tile_qwen2decoderlayer_pa_kernel(
         quantise((0, 3))
         fill_and_empty((1, 0), both_scalar)
         quantise(("h", 2))
-        rope = rope_tables(diagonals_k)
+        rope_k = rope_tables(diagonals_k)
         quantise(("h", 3))
         quantise((1, 0))
 
-        units = [(n, i) for n in range(GROUPS) for i in range(TOKEN_TILES)]
-
-        def at(beat):
-            return units[beat] if 0 <= beat < len(units) else (GROUPS, 0)
-
-        def finish(n, i):
-            scale_and_store(n, i, scale_scalar if i in SCALAR_TILES or n == LAST else scale_gpsimd)
-
         finish_at = {5:[[0,0]],6:[[0,1]],7:[[0,2]],8:[[0,3]],9:[[1,0]],10:[[1,1]],11:[[1,2]],12:[[1,3]],13:[[2,0]],14:[[2,1]],15:[[2,2]],16:[[2,3]],17:[[3,0]],18:[[3,1]],19:[[3,2],[3,3]],20:[[4,0],[4,1]],21:[[4,2],[4,3]]}
         for beat in range(len(units)):
-            unit = at(beat + PASSES + 1)
+            unit = at(beat + 5)
             n, i = at(beat)
-            last, tile = at(beat - 1) if beat > 0 else (GROUPS, 0)
+            last, tile = at(beat - 1)
             if unit[0] < GROUPS:
                 fill_and_empty(unit, both_scalar)
             project(n, i)
@@ -515,7 +521,7 @@ def tile_qwen2decoderlayer_pa_kernel(
             if n == V_GROUP:
                 store_plain(n, i)
             if last < V_GROUP:
-                rotate(last, rope if last == K_GROUP else rope_q, tile, tile + 1)
+                rotate(last, rope_k if last == K_GROUP else rope_q, tile, tile + 1)
             if unit[0] < GROUPS:
                 quantise(unit)
             if beat == 19:
@@ -530,4 +536,4 @@ def tile_qwen2decoderlayer_pa_kernel(
                 if last == LAST and tile % HALF_TILES == 1:
                     head_root(last, tile - 1, tile + 1)
             for done, j in finish_at.get(beat, []):
-                finish(done, j)
+                scale_and_store(done, j, (3,) if done < 2 else ())

from contextlib import ExitStack

import concourse.mybir as mybir
from concourse.masks import make_identity

F32 = mybir.dt.float32
BF16 = mybir.dt.bfloat16
I32 = mybir.dt.int32
U32 = mybir.dt.uint32
U8 = mybir.dt.uint8
FP8X4 = mybir.dt.float8_e4m3fn_x4
ACT = mybir.ActivationFunctionType
ALU = mybir.AluOpType

P = 128
TOKENS = 512
HID = 2048
HEAD = 128
HALF = HEAD // 2
EPS = 1e-6

TOKEN_TILES = TOKENS // P
PACK = 4
K_PASS = P * PACK
PASSES = HID // K_PASS
PAIR = 2
PASS_WORDS = K_PASS // PAIR
WORDS = PACK // PAIR
GROUP = 512
GROUP_HEADS = GROUP // HEAD
ROW_TILES = GROUP // P
Q_GROUPS = 4
GROUPS = Q_GROUPS + 2
K_GROUP = 0
V_GROUP = GROUPS - 1
LAST = V_GROUP - 1

WEIGHT_BUFS = 4
RING_BANKS = 6
UNIT_BANKS = 2
RUN_AHEAD = RING_BANKS // UNIT_BANKS
BANK_PASSES = PASSES // UNIT_BANKS
BANK_ROW_TILES = ROW_TILES // UNIT_BANKS
BANK_BF16 = 1024

ROW_GAIN_K = HID
ROW_GAIN_Q = ROW_GAIN_K + HEAD
ROW_LENGTH = ROW_GAIN_Q + HEAD
ROTATE_TILES = 2
HALF_TILES = TOKEN_TILES // 2

FLOPS = 2 * TOKENS * HID * GROUPS * GROUP


def tile_qwen2decoderlayer_pa_kernel(
    tc, x, cos, sin, wq, bq, wk, bk, wv, bv, q_norm_w, k_norm_w, ln1_w, out_0, out_1, out_2
):
    nc = tc.nc

    q_flat = out_0.rearrange("(p i) a d -> p i (a d)", i=TOKEN_TILES)
    q_slices = [slice(n * GROUP, (n + 1) * GROUP) for n in range(Q_GROUPS)]
    weight_rows = [wk] + [wq[cols, :] for cols in q_slices] + [wv]
    out_cols = (
        [out_1.rearrange("(p i) a d -> p i (a d)", i=TOKEN_TILES)]
        + [q_flat[:, :, cols] for cols in q_slices]
        + [out_2.rearrange("(p i) a d -> p i (a d)", i=TOKEN_TILES)]
    )

    with ExitStack() as ctx:
        ctx.enter_context(tc.manual_schedule())
        const = ctx.enter_context(tc.tile_pool(name="const", bufs=1))
        hpool = ctx.enter_context(tc.tile_pool(name="hpool", bufs=TOKEN_TILES))
        wpool = ctx.enter_context(tc.tile_pool(name="wpool", bufs=2 * WEIGHT_BUFS))
        gpool = ctx.enter_context(tc.tile_pool(name="gpool", bufs=6))
        cpool = ctx.enter_context(tc.tile_pool(name="cpool", bufs=2))
        epool = ctx.enter_context(tc.tile_pool(name="epool", bufs=2))
        stats = ctx.enter_context(tc.tile_pool(name="stats", bufs=2))
        ring = ctx.enter_context(tc.psum_pool(name="ring", bufs=RING_BANKS))
        table_psum = ctx.enter_context(tc.psum_pool(name="table_psum", bufs=1))

        x_sb = const.tile([P, TOKEN_TILES, HID], BF16)
        x_rows = x.rearrange("(p i) k -> p i k", i=TOKEN_TILES)
        nc.sync.dma_start(out=x_sb[:, 0, :], in_=x_rows[:, 0, :])
        row = const.tile([P, ROW_LENGTH], BF16)
        nc.vector.memset(row[:].bitcast(I32), 0)

        def load_row(first, vector):
            nc.sync.dma_start(out=row[0:1, first : first + vector.shape[0]], in_=vector.unsqueeze(0))

        load_row(0, ln1_w)
        load_row(ROW_GAIN_K, k_norm_w)
        load_row(ROW_GAIN_Q, q_norm_w)
        nc.sync.dma_start(out=x_sb[:, 1, :], in_=x_rows[:, 1, :])

        w_sb = {}

        def load_weights(n):
            halves = []
            for half in range(2):
                rows = slice(half * GROUP // 2, (half + 1) * GROUP // 2)
                w_half = wpool.tile([P, ROW_TILES // 2, HID], BF16, tag="w_half")
                nc.sync.dma_start(out=w_half[:], in_=weight_rows[n][rows, :].rearrange("(r p) k -> p r k", p=P))
                halves.append(w_half)
            w_sb[n] = halves

        def load_features(n, half):
            w_half = wpool.tile([P, ROW_TILES, HID // 2], BF16, tag="w_half")
            nc.sync.dma_start(
                out=w_half[:],
                in_=weight_rows[n][:, half * HID // 2 : (half + 1) * HID // 2].rearrange("(r p) k -> p r k", p=P),
            )
            w_sb.setdefault(n, []).append(w_half)

        def weight_words(n, r, g):
            if n == 0:
                half, part = divmod(g, PASSES // 2)
                words = w_sb[n][half][:, r, :].bitcast(F32)
            else:
                half, r = divmod(r, ROW_TILES // 2)
                part = g
                words = w_sb[n][half][:, r, :].bitcast(F32)
            return words[:, part * PASS_WORDS : (part + 1) * PASS_WORDS]

        load_features(0, 0)
        for i in range(2, TOKEN_TILES):
            nc.sync.dma_start(out=x_sb[:, i, :], in_=x_rows[:, i, :])
        load_features(0, 1)
        cos_sin = const.tile([P, 2, TOKEN_TILES, HEAD], BF16)
        nc.sync.dma_start(out=cos_sin[:, 0, :, :], in_=cos.rearrange("(p i) d -> p i d", i=TOKEN_TILES))
        nc.sync.dma_start(out=cos_sin[:, 1, :, :], in_=sin.rearrange("(p i) d -> p i d", i=TOKEN_TILES))
        bias = const.tile([P, GROUPS * GROUP], BF16)
        load_weights(1)
        nc.sync.dma_start(out=bias[:, 0:GROUP], in_=bk.partition_broadcast(P))
        load_weights(2)
        nc.sync.dma_start(out=bias[:, GROUP : V_GROUP * GROUP], in_=bq.partition_broadcast(P))
        load_weights(3)
        nc.sync.dma_start(out=bias[:, V_GROUP * GROUP :], in_=bv.partition_broadcast(P))

        ident_f = const.tile([P, P], F32)
        make_identity(nc, ident_f[:])
        ident_bf = const.tile([P, P], BF16)
        make_identity(nc, ident_bf[:])
        eps = const.tile([P, 1], F32)
        nc.vector.memset(eps[:], EPS)
        warm = const.tile([P, 1], F32)
        nc.scalar.activation(out=warm[:], in_=eps[:], func=ACT.Sqrt)
        squares = const.tile([P, HID], BF16)

        ones = const.tile([P, P], BF16)
        nc.vector.memset(ones[:], 1.0)

        def spread(bank, first, width):
            for part in range(0, width, GROUP):
                end = min(part + GROUP, width)
                nc.tensor.matmul(
                    out=bank[:, part:end], lhsT=ones[:], rhs=row[:, first + part : first + end],
                    start=True, stop=True,
                )

        lnw_banks = []
        for half in range(UNIT_BANKS):
            bank = table_psum.tile([P, BANK_BF16], BF16, tag="table%d" % half, name="lnw_bank")
            spread(bank, half * BANK_BF16, BANK_BF16)
            lnw_banks.append(bank)

        gains = const.tile([P, 2 * HEAD], BF16)
        gain_k = gains[:, 0:HEAD]
        gain_q = gains[:, HEAD : 2 * HEAD]

        def spread_gains():
            bank = ring.tile([P, BANK_BF16], BF16, tag="bank")
            spread(bank, ROW_GAIN_K, 2 * HEAD)
            nc.vector.tensor_copy(out=gains[:], in_=bank[:, 0 : 2 * HEAD])

        h_codes = const.tile([P, TOKEN_TILES, PASSES, P], U32, align_bytes=64)
        h_scales = const.tile([P, TOKEN_TILES, PASSES, P], U8, align_bytes=64)
        x_ss = const.tile([P, TOKEN_TILES], F32)
        x_rms = const.tile([P, TOKEN_TILES], F32)
        x_rstd = const.tile([P, TOKEN_TILES], F32)
        rest = const.tile([P, 1], F32)
        squares_v = const.tile([P, HID // 2], BF16)
        h_tiles = {}
        banks = {}
        grouped = {}

        def x_squares(i):
            end = HID // 2 if i == 0 else HID
            nc.scalar.activation(
                out=squares[:, 0:end], in_=x_sb[:, i, 0:end], func=ACT.Square, accum_out=x_ss[:, i : i + 1]
            )
            if i == 0:
                nc.vector.scalar_tensor_tensor(
                    out=squares_v[:], in0=x_sb[:, i, end:HID], scalar=1.0, in1=x_sb[:, i, end:HID],
                    op0=ALU.mult, op1=ALU.mult, accum_out=rest[:],
                )
                nc.vector.tensor_scalar(
                    out=rest[:], in0=rest[:], scalar1=1.0 / HID, scalar2=EPS, op0=ALU.mult, op1=ALU.add
                )

        def x_root(i):
            nc.scalar.activation(
                out=x_rms[:, i : i + 1], in_=x_ss[:, i : i + 1], func=ACT.Sqrt,
                scale=1.0 / HID, bias=rest[:] if i == 0 else eps[:],
            )

        def word_order(row):
            return row.rearrange("p (g j u e) -> p u g j e", j=P, u=WORDS, e=PAIR)

        def x_scale(i):
            nc.vector.reciprocal(out=x_rstd[:, i : i + 1], in_=x_rms[:, i : i + 1])
            h_tile = hpool.tile([P, PASSES, WORDS, P, PAIR], BF16)
            for half in range(UNIT_BANKS):
                x_words = word_order(x_sb[:, i, half * BANK_BF16 : (half + 1) * BANK_BF16])
                lnw_words = word_order(lnw_banks[half][:])
                for u in range(WORDS):
                    nc.vector.scalar_tensor_tensor(
                        out=h_tile[:, half * BANK_PASSES : (half + 1) * BANK_PASSES, u, :, :],
                        in0=x_words[:, u, :, :, :], scalar=x_rstd[:, i : i + 1],
                        in1=lnw_words[:, u, :, :, :], op0=ALU.mult, op1=ALU.mult,
                    )
            h_tiles[i] = h_tile

        def transpose_h(i):
            words = h_tiles[i][:].rearrange("p g u j e -> p (g u j e)").bitcast(F32)
            for half in range(UNIT_BANKS):
                h_t = ring.tile([P, BANK_PASSES, WORDS, P], F32, tag="bank")
                for b in range(BANK_PASSES * WORDS):
                    g, u = divmod(b, WORDS)
                    first = (half * BANK_PASSES * WORDS + b) * P
                    nc.tensor.transpose(h_t[:, g, u, :], words[:, first : first + P], ident_f[:])
                banks[("h", i, half)] = h_t

        def copy_h(i, copies):
            tile = gpool.tile([P, GROUP * PACK], BF16, align_bytes=64, tag="grouped")
            words = tile[:].bitcast(F32).rearrange("p (g m u) -> p g m u", g=PASSES, u=WORDS)
            for half, copy in enumerate(copies):
                copy(
                    out=words[:, half * BANK_PASSES : (half + 1) * BANK_PASSES, :, :],
                    in_=banks[("h", i, half)][:].rearrange("p g u m -> p g m u"),
                )
            grouped[("h", i)] = tile

        def quantise_h(i):
            nc.vector.quantize_mx(
                out=h_codes[:, i, :, :].rearrange("p g m -> p (g m)").bitcast(FP8X4),
                scales=h_scales[:, i, :, :].rearrange("p g m -> p (g m)"),
                in_=grouped[("h", i)][:],
            )

        def diagonals(gain, name):
            swapped = const.tile([P, HEAD], BF16, name="swapped_" + name)
            nc.gpsimd.tensor_scalar(
                out=swapped[:, 0:HALF], in0=gain[:, HALF:HEAD], scalar1=-1.0, scalar2=0.0,
                op0=ALU.mult, op1=ALU.add,
            )
            nc.gpsimd.tensor_scalar(
                out=swapped[:, HALF:HEAD], in0=gain[:, 0:HALF], scalar1=1.0, scalar2=0.0,
                op0=ALU.mult, op1=ALU.add,
            )
            pair = const.tile([P, 2, HEAD], BF16, name="diagonals_" + name)
            nc.gpsimd.tensor_tensor(out=pair[:, 0, :], in0=ident_bf[:], in1=gain, op=ALU.mult)
            nc.gpsimd.tensor_tensor(out=pair[:, 1, :], in0=ident_bf[:], in1=swapped[:], op=ALU.mult)
            return pair

        turned = const.tile([P, 2, TOKEN_TILES, P], BF16)

        def turn_cos_sin():
            bank = ring.tile([P, 2, TOKEN_TILES, P], BF16, tag="bank")
            for half in range(2):
                for i in range(TOKEN_TILES):
                    nc.tensor.transpose(bank[:, half, i, :], cos_sin[:, half, i, :], ident_bf[:])
            nc.scalar.copy(out=turned[:], in_=bank[:])

        def rope_tables(pair, warm=0):
            in_psum = []
            for half in range(2):
                bank = table_psum.tile([P, TOKEN_TILES, HEAD], F32, tag="table%d" % half, name="rope_bank")
                for part in range(warm):
                    nc.tensor.matmul(
                        out=bank[:].rearrange("p i d -> p (i d)"), lhsT=ones[:], rhs=row[:, 0:GROUP],
                        start=True, stop=True,
                    )
                for i in range(TOKEN_TILES):
                    nc.tensor.matmul(
                        out=bank[:, i, :], lhsT=turned[:, half, i, :], rhs=pair[:, half, :],
                        start=True, stop=True,
                    )
                in_psum.append(bank)
            return in_psum

        w_codes = {}
        w_scales = {}
        sums = {}
        u_sb = {}
        straight = {}
        crossed = {}
        ss = {}
        rms_sb = {}
        rstd = {}

        def transpose_weights(n, g, warm=0):
            for rp in range(UNIT_BANKS):
                w_t = ring.tile([P, WORDS, BANK_ROW_TILES * P], F32, tag="bank")
                for part in range(warm if rp == 0 else 0):
                    nc.tensor.matmul(
                        out=w_t[:].rearrange("p u f -> p (u f)"), lhsT=ones[:], rhs=row[:, 0:GROUP],
                        start=True, stop=True,
                    )
                for u in range(WORDS):
                    for rr in range(BANK_ROW_TILES):
                        words = weight_words(n, BANK_ROW_TILES * rp + rr, g)
                        nc.tensor.transpose(
                            w_t[:, u, rr * P : (rr + 1) * P], words[:, u:PASS_WORDS:WORDS], ident_f[:]
                        )
                banks[(n, g, rp)] = w_t
            if g == PASSES - 1 and n + WEIGHT_BUFS < GROUPS:
                load_weights(n + WEIGHT_BUFS)

        def copy_weights(n, g, copies):
            tile = gpool.tile([P, GROUP * PACK], BF16, align_bytes=64, tag="grouped")
            words = tile[:].bitcast(F32).rearrange("p (f u) -> p f u", u=WORDS)
            bank_features = BANK_ROW_TILES * P
            for rp, copy in enumerate(copies):
                copy(
                    out=words[:, rp * bank_features : (rp + 1) * bank_features, :],
                    in_=banks[(n, g, rp)][:].rearrange("p u f -> p f u"),
                )
            grouped[(n, g)] = tile

        def quantise_weights(n, g):
            if g == 0:
                codes = cpool.tile([P, PASSES, GROUP], U32, align_bytes=64)
                scales = cpool.tile([P, PASSES, GROUP], U8, align_bytes=64)
                w_codes[n] = codes
                w_scales[n] = scales
            nc.vector.quantize_mx(
                out=w_codes[n][:, g, :].bitcast(FP8X4), scales=w_scales[n][:, g, :],
                in_=grouped[(n, g)][:],
            )

        def project(n, i):
            bank = ring.tile([P, GROUP], F32, tag="bank")
            for g in range(PASSES):
                nc.tensor.matmul_mx(
                    out=bank[:],
                    lhsT=h_codes[:, i, g, :].bitcast(FP8X4),
                    lhsT_scale=h_scales[:, i, g, :],
                    rhs=w_codes[n][:, g, :].bitcast(FP8X4),
                    rhs_scale=w_scales[n][:, g, :],
                    start=(g == 0),
                    stop=(g == PASSES - 1),
                )
            sums[(n, i)] = bank

        def add_bias(n, i):
            if i == 0:
                u = epool.tile([P, TOKEN_TILES, GROUP_HEADS, HEAD], F32)
                u_sb[n] = u
            nc.vector.tensor_tensor(
                out=u_sb[n][:, i, :, :].rearrange("p a d -> p (a d)"), in0=sums[(n, i)][:],
                in1=bias[:, n * GROUP : (n + 1) * GROUP], op=ALU.add,
            )

        def head_squares(n, i):
            if i == 0:
                sums_of_squares = stats.tile([P, TOKEN_TILES * GROUP_HEADS], F32)
                ss[n] = sums_of_squares
            for head in range(GROUP_HEADS):
                col = i * GROUP_HEADS + head
                nc.scalar.activation(
                    out=squares[:, col * HEAD : (col + 1) * HEAD], in_=u_sb[n][:, i, head, :],
                    func=ACT.Square, accum_out=ss[n][:, col : col + 1],
                )

        def head_root(n, first, last):
            cols = slice(first * GROUP_HEADS, last * GROUP_HEADS)
            if first == 0:
                rms = stats.tile([P, TOKEN_TILES * GROUP_HEADS], F32)
                rms_sb[n] = rms
            nc.scalar.activation(
                out=rms_sb[n][:, cols], in_=ss[n][:, cols], func=ACT.Sqrt, scale=1.0 / HEAD, bias=eps[:, 0:1]
            )

        def invert_rms(n, first, last):
            cols = slice(first * GROUP_HEADS, last * GROUP_HEADS)
            if first == 0:
                inv = stats.tile([P, TOKEN_TILES * GROUP_HEADS], F32)
                rstd[n] = inv
            nc.vector.reciprocal(out=rstd[n][:, cols], in_=rms_sb[n][:, cols])

        def rotate(n, tables, first, last):
            cos_gain, sin_gain = tables
            if first == 0:
                by_cos = epool.tile([P, TOKEN_TILES, GROUP_HEADS, HEAD], F32, bufs=3)
                by_sin = epool.tile([P, TOKEN_TILES, GROUP_HEADS, HEAD], F32, bufs=1)
                straight[n] = by_cos
                crossed[n] = by_sin
            tiles = slice(first, last)
            shape = [P, last - first, GROUP_HEADS, HEAD]
            half_shape = [P, last - first, GROUP_HEADS, HALF]
            u = u_sb[n]
            nc.vector.tensor_tensor(
                out=straight[n][:, tiles, :, :], in0=u[:, tiles, :, :],
                in1=cos_gain[:, tiles, :].unsqueeze(2).to_broadcast(shape), op=ALU.mult,
            )
            nc.vector.tensor_tensor(
                out=crossed[n][:, tiles, :, 0:HALF], in0=u[:, tiles, :, HALF:HEAD],
                in1=sin_gain[:, tiles, 0:HALF].unsqueeze(2).to_broadcast(half_shape), op=ALU.mult,
            )
            nc.vector.tensor_tensor(
                out=crossed[n][:, tiles, :, HALF:HEAD], in0=u[:, tiles, :, 0:HALF],
                in1=sin_gain[:, tiles, HALF:HEAD].unsqueeze(2).to_broadcast(half_shape), op=ALU.mult,
            )
            for i in range(first, last):
                nc.gpsimd.tensor_tensor(
                    out=straight[n][:, i, :, :], in0=straight[n][:, i, :, :], in1=crossed[n][:, i, :, :],
                    op=ALU.add,
                )

        def scale_scalar(n, i, head):
            col = i * GROUP_HEADS + head
            nc.scalar.activation(
                out=straight[n][:, i, head, :], in_=straight[n][:, i, head, :], func=ACT.Copy,
                scale=rstd[n][:, col : col + 1],
            )

        def scale_gpsimd(n, i, head):
            col = i * GROUP_HEADS + head
            nc.gpsimd.tensor_scalar(
                out=straight[n][:, i, head, :], in0=straight[n][:, i, head, :],
                scalar1=rstd[n][:, col : col + 1], scalar2=0.0, op0=ALU.mult, op1=ALU.add,
            )

        def scale_and_store(n, i, gpsimd_heads):
            for head in range(GROUP_HEADS):
                scale = scale_gpsimd if head in gpsimd_heads else scale_scalar
                scale(n, i, head)
            nc.sync.dma_start(
                out=out_cols[n][:, i, :],
                in_=straight[n][:, i, :, :].rearrange("p a d -> p (a d)"),
            )

        def store_plain(n, i):
            nc.sync.dma_start(
                out=out_cols[n][:, i, :],
                in_=u_sb[n][:, i, :, :].rearrange("p a d -> p (a d)"),
            )

        both_scalar = (nc.scalar.copy, nc.scalar.copy)
        both_vector = (nc.vector.tensor_copy, nc.vector.tensor_copy)
        one_each = (nc.scalar.copy, nc.vector.tensor_copy)

        def fill_and_empty(unit, copies, warm=0):
            kind, part = unit
            if kind == "h":
                transpose_h(part)
                copy_h(part, copies)
            else:
                transpose_weights(kind, part, warm)
                copy_weights(kind, part, copies)

        def quantise(unit):
            kind, part = unit
            if kind == "h":
                quantise_h(part)
            else:
                quantise_weights(kind, part)

        units = [(n, i) for n in range(GROUPS) for i in range(TOKEN_TILES)]

        def at(beat):
            return units[beat] if 0 <= beat < len(units) else (GROUPS, 0)

        x_squares(0)
        x_root(0)
        x_squares(1)
        x_root(1)
        x_squares(2)
        x_root(2)
        x_squares(3)
        x_root(3)
        spread_gains()
        diagonals_k = diagonals(gain_k, "k")
        diagonals_q = diagonals(gain_q, "q")
        x_scale(0)
        x_scale(1)
        fill_and_empty((0, 0), both_vector)
        fill_and_empty(("h", 0), both_scalar)
        fill_and_empty((0, 1), both_scalar)
        x_scale(2)
        x_scale(3)
        fill_and_empty(("h", 1), both_scalar)
        quantise((0, 0))
        quantise(("h", 0))
        fill_and_empty((0, 2), both_scalar)
        quantise((0, 1))
        fill_and_empty((0, 3), both_scalar)
        quantise(("h", 1))
        fill_and_empty(("h", 2), one_each)
        quantise((0, 2))
        turn_cos_sin()
        fill_and_empty(("h", 3), one_each)
        quantise((0, 3))
        fill_and_empty((1, 0), both_scalar)
        quantise(("h", 2))
        rope_k = rope_tables(diagonals_k)
        quantise(("h", 3))
        quantise((1, 0))

        finish_at = {5:[[0,0]],6:[[0,1]],7:[[0,2]],8:[[0,3]],9:[[1,0]],10:[[1,1]],11:[[1,2]],12:[[1,3]],13:[[2,0]],14:[[2,1]],15:[[2,2]],16:[[2,3]],17:[[3,0]],18:[[3,1]],19:[[3,2],[3,3]],20:[[4,0],[4,1]],21:[[4,2],[4,3]]}
        for beat in range(len(units)):
            unit = at(beat + 5)
            n, i = at(beat)
            last, tile = at(beat - 1)
            if unit[0] < GROUPS:
                fill_and_empty(unit, both_scalar)
            project(n, i)
            if beat == PASSES + 1:
                rope_q = rope_tables(diagonals_q)
            add_bias(n, i)
            if n == V_GROUP:
                store_plain(n, i)
            if last < V_GROUP:
                rotate(last, rope_k if last == K_GROUP else rope_q, tile, tile + 1)
            if unit[0] < GROUPS:
                quantise(unit)
            if beat == 19:
                invert_rms(LAST, 0, HALF_TILES)
            if beat == 21:
                invert_rms(LAST, HALF_TILES, TOKEN_TILES)
            if last < V_GROUP:
                head_squares(last, tile)
                if last < LAST and tile == TOKEN_TILES - 1:
                    head_root(last, 0, TOKEN_TILES)
                    invert_rms(last, 0, TOKEN_TILES)
                if last == LAST and tile % HALF_TILES == 1:
                    head_root(last, tile - 1, tile + 1)
            for done, j in finish_at.get(beat, []):
                scale_and_store(done, j, (3,) if done < 2 else ())
